import numpy as np
import ml_dtypes


def mxq(x, axis, fmt="e4m3"):
    dtype, down = {"e4m3": (ml_dtypes.float8_e4m3fn, 7), "e5m2": (ml_dtypes.float8_e5m2, 14)}[fmt]
    v = np.moveaxis(np.asarray(x, np.float32).astype(ml_dtypes.bfloat16).astype(np.float64), axis, -1)
    blocks = v.reshape(v.shape[:-1] + (-1, 32))
    amax = np.abs(blocks).max(-1, keepdims=True)
    byte = np.maximum(np.where(amax > 0, np.frexp(amax)[1] - 1 + 127, 0) - down, 1)
    scale = np.exp2(byte - 127.0)
    codes = (blocks / scale).astype(np.float32).astype(dtype).astype(np.float64)
    return np.moveaxis((codes * scale).reshape(v.shape), -1, axis)


WIDE = False


def mx_kscale(k):
    if not WIDE:
        return np.ones(k)
    levels = np.array([10, -10, 5, -5, 0])
    if k % 512:
        return np.exp2(np.random.permutation(np.resize(levels, k // 32))).repeat(32)
    a = np.empty((k // 512, 16))
    for p in range(k // 512):
        a[p, :8] = np.random.permutation(np.resize(levels, 8))
        for g in range(8):
            far = levels[np.abs(levels - a[p, g]) >= 10]
            a[p, g + 8] = far[np.random.randint(len(far))]
    return np.exp2(a.ravel()).repeat(32)


BF16 = ml_dtypes.bfloat16


def bf(x):
    return np.asarray(x, np.float32).astype(BF16)


def f64(x):
    return np.asarray(x).astype(np.float64)


DIM, H, HKV, D, B, S = 1024, 16, 4, 128, 2, 512
T = B * S


def rope_table():
    inv_freq = 1.0 / (10000.0 ** (np.arange(0, D, 2) / D))
    ang = np.arange(S)[:, None] * inv_freq[None, :]
    fc = np.stack([np.cos(ang), np.sin(ang)], axis=-1)
    return np.tile(fc, (B, 1, 1))


def rope(t, fc):
    t2 = t.reshape(t.shape[0], t.shape[1], D // 2, 2)
    cos = fc[:, None, :, 0]
    sin = fc[:, None, :, 1]
    r0 = t2[..., 0] * cos - t2[..., 1] * sin
    r1 = t2[..., 0] * sin + t2[..., 1] * cos
    return np.stack([r0, r1], axis=-1).reshape(t.shape)


def draw0():
    s = mx_kscale(DIM)
    return {"x": bf(np.random.standard_normal((T, DIM)) * s),
            "freqs_cis": bf(rope_table()),
            "wq": bf(np.random.standard_normal((DIM, H * D)) * 1.5 / np.sqrt(DIM) / s[:, None]),
            "wk": bf(np.random.standard_normal((DIM, HKV * D)) * 1.5 / np.sqrt(DIM) / s[:, None]),
            "wv": bf(np.random.standard_normal((DIM, HKV * D)) / np.sqrt(DIM) / s[:, None])}


def core(x, freqs_cis, wq, wk, wv):
    xq = mxq(f64(x), 1, "e4m3")
    fc = f64(freqs_cis)
    q_rot = rope((xq @ mxq(f64(wq), 0, "e4m3")).reshape(T, H, D), fc)
    k_rot = rope((xq @ mxq(f64(wk), 0, "e4m3")).reshape(T, HKV, D), fc)
    v = (xq @ mxq(f64(wv), 0, "e4m3")).reshape(T, HKV, D)
    return q_rot, k_rot, v


def e4m3fn_bytes(y):
    return np.clip(np.asarray(y, np.float64), -448.0, 448.0).astype(np.float32).astype(ml_dtypes.float8_e4m3fn).view(np.uint8)


def e4m3fn_values(b):
    return np.asarray(b, np.uint8).view(ml_dtypes.float8_e4m3fn).astype(np.float64)


def setup_inputs():
    d = draw0()
    x0 = np.asarray(d['wq']).astype(np.float64)
    s = (np.max(np.abs(x0), axis=(1,), keepdims=True) / 448.0).astype(np.float32)
    out = {}
    for k, v in d.items():
        if k == 'wq':
            out['wq_bytes'] = e4m3fn_bytes(x0 / s.astype(np.float64))
            out['wq_scale'] = s
        else:
            out[k] = v
    return out


def reference(x, freqs_cis, wq_bytes, wq_scale, wk, wv):
    return core(x, freqs_cis, e4m3fn_values(wq_bytes) * wq_scale.astype(np.float64), wk, wv)

@@ -1,0 +1,267 @@
+from contextlib import ExitStack
+
+import concourse.mybir as mybir
+from concourse.masks import make_identity
+
+F32 = mybir.dt.float32
+BF16 = mybir.dt.bfloat16
+U32 = mybir.dt.uint32
+U8 = mybir.dt.uint8
+FP8 = mybir.dt.float8_e4m3fn
+FP8X4 = mybir.dt.float8_e4m3fn_x4
+MULT = mybir.AluOpType.mult
+ADD = mybir.AluOpType.add
+SUB = mybir.AluOpType.subtract
+COPY = mybir.ActivationFunctionType.Copy
+
+P = 128
+TOKENS, DIM = 1024, 1024
+NT = TOKENS // P
+NG = DIM // 512
+CW = 512
+HW = CW // 2
+NH = 4
+FLOPS = 2 * TOKENS * DIM * 3072
+
+LOADS = "k x0 f x1 x2 x3 sc q1 x4 x5 x6 x7 q2 q3 q4 v"
+XGROUPS = ((0, 1), (2, 3), (4, 5, 6, 7))
+HEAD = ("I0.0.S.0.176 I0.0.V.176.512 I0.1.S.0.176 I0.1.V.176.512 T0 E0.S T1 E1.S W0 F T2 E2.S T3 E3.S X0 M0 M1 P P T4 E4.S T5 E5.S K0 X1 M2 M3 T6 P P E6.S T7 E7.S K1 K2 X2 A0.V M4 M5 K3 A1.G M6 M7 P P P P K4 K5 A2.G K6 K7 P* W1 M8 M9 A3.V")
+CHUNK = "P P P M+2 M+3 K0 K1 A0.G P P P M+4 M+5 K2 K3 A1.G P P P M+6 M+7 K4 K5 A2.G P P P K6 K7 P* W+ M+8 M+9 A3.V"
+LAST = "P P M+2 M+3 K0 K1 A0.G P P M+4 M+5 K2 K3 P* W+ A1.V M+6 M+7 V V K4 V K5 A2.G V K6 V V K7 B6.V B7.V V V"
+BUFS = 4
+
+
+def tile_attention_pa_kernel(tc, x, freqs_cis, wq_bytes, wq_scale, wk, wv, out_0, out_1, out_2):
+    nc = tc.nc
+    with ExitStack() as ctx:
+        const = ctx.enter_context(tc.tile_pool(name="const", bufs=1))
+        raw = ctx.enter_context(tc.tile_pool(name="raw", bufs=1))
+        stage = ctx.enter_context(tc.tile_pool(name="stage", bufs=3))
+        codes = ctx.enter_context(tc.tile_pool(name="codes", bufs=1))
+        prod = ctx.enter_context(tc.tile_pool(name="prod", bufs=BUFS))
+        psum_a = ctx.enter_context(tc.psum_pool(name="psum_a", bufs=6))
+        psum_x = ctx.enter_context(tc.psum_pool(name="psum_x", bufs=2))
+        ctx.enter_context(tc.manual_schedule())
+
+        wk_v = wk.rearrange("(g p j) n -> g p j n", p=P, j=4)
+        wv_v = wv.rearrange("(g p j) n -> g p j n", p=P, j=4)
+        wq_v = wq_bytes.rearrange("(g p j) n -> g p j n", p=P, j=4)
+        fc_v = freqs_cis.rearrange("(p i) j c -> p i (j c)", i=NT)
+        x_v = x.rearrange("(p i) k -> i p k", i=NT)
+        q_out = out_0.rearrange("(p i) h d -> p i (h d)", i=NT)
+        k_out = out_1.rearrange("(p i) h d -> p i (h d)", i=NT)
+        v_out = out_2.rearrange("(p i) h d -> p i (h d)", i=NT)
+
+        wraw, wqb, x_raw = {}, {}, {}
+        fc = const.tile([P, NT, P], BF16, name="fc")
+        sc = const.tile([P, NG, 4], F32, name="sc")
+        for item in LOADS.split():
+            if item in ("k", "v"):
+                c, view = (0, wk_v) if item == "k" else (5, wv_v)
+                for g in range(NG):
+                    wraw[c, g] = raw.tile([P, 4, CW], BF16, name="wraw%d_%d" % (c, g))
+                    nc.sync.dma_start(out=wraw[c, g], in_=view[g])
+            elif item[0] == "q":
+                c = int(item[1])
+                for g in (range(NG) if len(item) == 2 else (int(item[2]),)):
+                    wqb[c, g] = raw.tile([P, 4, CW], U8, name="wq_bytes%d_%d" % (c, g))
+                    nc.sync.dma_start(out=wqb[c, g], in_=wq_v[g][:, :, (c - 1) * CW:c * CW])
+            elif item[0] == "x":
+                i = int(item[1])
+                x_raw[i] = raw.tile([P, DIM], BF16, name="x_raw%d" % i)
+                nc.sync.dma_start(out=x_raw[i], in_=x_v[i])
+            elif item == "f":
+                nc.sync.dma_start(out=fc, in_=fc_v)
+            else:
+                nc.sync.dma_start(out=sc, in_=wq_scale.rearrange("(g p j) o -> p g (j o)", p=P, j=4))
+
+        ident = const.tile([P, P], F32, name="ident")
+        make_identity(nc, ident[:])
+        warm = const.tile([P, 2], F32, name="warm")
+        nc.vector.memset(warm[:, 0:1], 0.0)
+        nc.scalar.activation(out=warm[:, 1:2], in_=warm[:, 0:1], func=COPY)
+        s2 = const.tile([P, NT, 2, 64], BF16, name="s2")
+
+        def tables(i0, i1):
+            sin = fc[:, i0:i1, :].rearrange("p i (j c) -> p i j c", c=2)[:, :, :, 1]
+            nc.vector.tensor_scalar(out=s2[:, i0:i1, 0, :], in0=sin, scalar1=-1.0, scalar2=None, op0=MULT)
+            nc.vector.tensor_copy(out=s2[:, i0:i1, 1, :], in_=sin)
+
+        xt, xg, xc, xs = {}, {}, {}, {}
+
+        def x_transpose(i):
+            xt[i] = psum_x.tile([P, NG, 2, P], F32, name="xt")
+            words = x_raw[i].bitcast(F32)
+            for g in range(NG):
+                for u in range(2):
+                    nc.tensor.transpose(xt[i][:, g, u, :], words[:, 256 * g + u:256 * (g + 1):2], ident)
+
+        where = {}
+        for n, grp in enumerate(XGROUPS):
+            for pos, i in enumerate(grp):
+                where[i] = (n, pos)
+
+        def x_evacuate(i, eng):
+            n, pos = where[i]
+            if pos == 0:
+                xg[n] = stage.tile([P, len(XGROUPS[n]), 2 * CW], BF16, name="xg%d" % n, align_bytes=64, bufs=1)
+            dst = xg[n][:, pos, :].bitcast(F32).rearrange("p (g r u) -> p g r u", g=NG, u=2)
+            src = xt[i].rearrange("p g u r -> p g r u")
+            if eng == "V":
+                nc.vector.tensor_copy(out=dst, in_=src)
+            else:
+                nc.scalar.copy(out=dst, in_=src)
+
+        def x_quantise(n):
+            width = len(XGROUPS[n]) * NG * P
+            xc[n] = codes.tile([P, width], U32, name="xc%d" % n, align_bytes=64)
+            xs[n] = codes.tile([P, width], U8, name="xs%d" % n, align_bytes=64)
+            nc.vector.quantize_mx(out=xc[n].bitcast(FP8X4), scales=xs[n], in_=xg[n].rearrange("p a k -> p (a k)"))
+
+        wg, wc, ws, wide = {}, {}, {}, {}
+
+        def interleave(eng, c, g, n0, n1):
+            if c not in wg:
+                wg[c] = stage.tile([P, NG, CW, 4], BF16, name="wg", align_bytes=64)
+            src = wide[c, g] if (c, g) in wide else wraw[c, g]
+            dst = wg[c][:, g, n0:n1, :]
+            s = src[:, :, n0:n1].rearrange("p t n -> p n t")
+            if eng == "V":
+                nc.vector.tensor_copy(out=dst, in_=s)
+            elif eng == "S":
+                nc.scalar.copy(out=dst, in_=s)
+            else:
+                nc.gpsimd.tensor_scalar(out=dst, in0=s, scalar1=1.0, scalar2=0.0, op0=MULT, op1=ADD)
+
+        def widen(c, g, j):
+            if j == 0:
+                wide[c, g] = stage.tile([P, 4, CW], BF16, name="wide")
+            nc.scalar.activation(out=wide[c, g][:, j, :], in_=wqb[c, g][:, j, :].bitcast(FP8), func=COPY,
+                                 scale=sc[:, g, j:j + 1])
+
+        def w_quantise(c):
+            wc[c] = codes.tile([P, NG * CW], U32, name="wc%d" % c, align_bytes=64)
+            ws[c] = codes.tile([P, NG * CW], U8, name="ws%d" % c, align_bytes=64)
+            nc.vector.quantize_mx(out=wc[c].bitcast(FP8X4), scales=ws[c],
+                                  in_=wg[c].rearrange("p g n j -> p (g n j)"))
+
+        def mx(out, c, i, g, n0, n1, start, stop):
+            n, pos = where[i]
+            cols = slice((pos * NG + g) * P, (pos * NG + g + 1) * P)
+            w = slice(g * CW + n0, g * CW + n1)
+            nc.tensor.matmul_mx(out=out, lhsT=xc[n][:, cols].bitcast(FP8X4), lhsT_scale=xs[n][:, cols],
+                                rhs=wc[c][:, w].bitcast(FP8X4), rhs_scale=ws[c][:, w], start=start, stop=stop)
+
+        acc = {}
+
+        def bank_matmuls(b):
+            c, i = b // NT, b % NT
+            acc[c, i] = psum_a.tile([P, CW], F32, name="acc")
+            for g in range(NG):
+                mx(acc[c, i], c, i, g, 0, CW, g == 0, g == NG - 1)
+
+        p1, p2 = {}, {}
+
+        def shape4(ap):
+            return ap.rearrange("p (h j e) -> p h j e", h=NH, e=2)
+
+        def products(c, i):
+            u = 4 * c + i // 2
+            if i % 2 == 0:
+                p1[u] = prod.tile([P, 2, CW], F32, name="p1")
+                p2[u] = prod.tile([P, 2, CW], F32, name="p2")
+            full = [P, NH, 64, 2]
+            a4 = shape4(acc[c, i])
+            cosb = fc[:, i, :].rearrange("p (j c) -> p j c", c=2)[:, :, 0:1].unsqueeze(1).to_broadcast(full)
+            sinb = s2[:, i, :, :].rearrange("p e j -> p j e").unsqueeze(1).to_broadcast(full)
+            nc.vector.tensor_tensor(out=shape4(p1[u][:, i % 2, :]), in0=cosb, in1=a4, op=MULT)
+            nc.vector.tensor_tensor(out=shape4(p2[u][:, i % 2, :]), in0=sinb, in1=a4[:, :, :, ::-1], op=MULT)
+
+        def add_store(u, eng):
+            c, i0 = u // 4, 2 * (u % 4)
+            o = prod.tile([P, 2, CW], F32, name="o")
+            engine = nc.vector if eng == "V" else nc.gpsimd
+            engine.tensor_tensor(out=o, in0=p1[u], in1=p2[u], op=ADD)
+            dst = k_out[:, i0:i0 + 2, :] if c == 0 else q_out[:, i0:i0 + 2, (c - 1) * CW:c * CW]
+            nc.sync.dma_start(out=dst, in_=o)
+
+        def add_store_bank(c, i, eng):
+            u = 4 * c + i // 2
+            o = prod.tile([P, CW], F32, name="o1")
+            engine = nc.vector if eng == "V" else nc.gpsimd
+            engine.tensor_tensor(out=o, in0=p1[u][:, i % 2, :], in1=p2[u][:, i % 2, :], op=ADD)
+            dst = k_out[:, i, :] if c == 0 else q_out[:, i, (c - 1) * CW:c * CW]
+            nc.sync.dma_start(out=dst, in_=o)
+
+        work = []
+        for c in (1, 2, 3, 4, 5):
+            for g in range(NG):
+                if c < 5:
+                    for j in range(4):
+                        work.append(("widen", c, g, j))
+                for blk in range(2):
+                    work.append(("il", c, g, blk))
+        taken = [0]
+
+        def prep_one():
+            kind, c, g, a = work[taken[0]]
+            taken[0] += 1
+            if kind == "widen":
+                widen(c, g, a)
+            else:
+                interleave("S", c, g, a * HW, (a + 1) * HW)
+
+        def prep_chunk(c):
+            while taken[0] < len(work) and work[taken[0]][1] <= c:
+                prep_one()
+
+        vstate = {"n": 0}
+
+        def value_tile():
+            i = vstate["n"]
+            a = psum_x.tile([P, CW], F32, name="xt")
+            for g in range(NG):
+                mx(a, 5, i, g, 0, CW, g == 0, g == NG - 1)
+            if i % 2 == 0:
+                vstate["o"] = prod.tile([P, 2, CW], F32, name="vo")
+            nc.scalar.copy(out=vstate["o"][:, i % 2, :], in_=a)
+            if i % 2 == 1:
+                nc.scalar.dma_start(out=v_out[:, i - 1:i + 1, :], in_=vstate["o"])
+            vstate["n"] = i + 1
+
+        def run(program, c):
+            for tok in program.split():
+                op, arg = tok[0], tok[1:]
+                if op == "I":
+                    a = arg.split(".")
+                    interleave(a[2], int(a[0]), int(a[1]), int(a[3]), int(a[4]))
+                elif op == "T":
+                    x_transpose(int(arg))
+                elif op == "E":
+                    x_evacuate(int(arg[0]), arg[2])
+                elif op == "X":
+                    x_quantise(int(arg))
+                elif op == "F":
+                    tables(0, NT)
+                elif op == "W":
+                    w_quantise(c + 1 if arg == "+" else int(arg))
+                elif op == "M":
+                    bank_matmuls(NT * c + int(arg[1:]) if arg[0] == "+" else int(arg))
+                elif op == "K":
+                    products(c, int(arg))
+                elif op == "A":
+                    add_store(4 * c + int(arg[0]), arg[2])
+                elif op == "B":
+                    add_store_bank(c, int(arg[0]), arg[2])
+                elif op == "V":
+                    value_tile()
+                elif tok == "P":
+                    prep_one()
+                else:
+                    assert tok == "P*"
+                    prep_chunk(c + 1)
+
+        run(HEAD, 0)
+        for c in (1, 2, 3):
+            run(CHUNK, c)
+        run(LAST, 4)

@@ -25,9 +25,9 @@ FLOPS = 2 * TOKENS * DIM * 3072
 
 LOADS = "k x0 f x1 x2 x3 sc q1 x4 x5 x6 x7 q2 q3 q4 v"
 XGROUPS = ((0, 1), (2, 3), (4, 5, 6, 7))
-HEAD = ("I0.0.S.0.176 I0.0.V.176.512 I0.1.S.0.176 I0.1.V.176.512 T0 E0.S T1 E1.S W0 F T2 E2.S T3 E3.S X0 M0 M1 P P T4 E4.S T5 E5.S K0 X1 M2 M3 T6 P P E6.S T7 E7.S K1 K2 X2 A0.V M4 M5 K3 A1.G M6 M7 P P P P K4 K5 A2.G K6 K7 P* W1 M8 M9 A3.V")
-CHUNK = "P P P M+2 M+3 K0 K1 A0.G P P P M+4 M+5 K2 K3 A1.G P P P M+6 M+7 K4 K5 A2.G P P P K6 K7 P* W+ M+8 M+9 A3.V"
-LAST = "P P M+2 M+3 K0 K1 A0.G P P M+4 M+5 K2 K3 P* W+ A1.V M+6 M+7 V V K4 V K5 A2.G V K6 V V K7 B6.V B7.V V V"
+HEAD = ("I0.0.S.0.176 I0.0.V.176.512 I0.1.S.0.176 I0.1.V.176.512 T0 E0.S T1 E1.S W0 F T2 E2.S T3 E3.V X0 M0 M1 P P T4 E4.S T5 E5.S K0 X1 M2 M3 T6 P P T7 K1 K2 E6.V E7.V X2 A0.V M4 M5 K3 A1.G M6 M7 P P P P K4 B4.G K5 K6 C7 P* W1 M8 M9 B5.V")
+CHUNK = "D-7 A-3.G P P P M+2 M+3 K0 K1 A0.G P P P M+4 M+5 K2 K3 A1.G P P P M+6 M+7 K4 B4.G K5 P P P K6 C7 P* W+ M+8 M+9 B5.V"
+LAST = "D-7 A-3.G P P M+2 M+3 K0 K1 P* W+ A0.V M+4 M+5 V V K2 V K3 A1.G V M+6 M+7 K4 V V K5 A2.G V V K6 K7 B6.V B7.V"
 BUFS = 4
 
 
@@ -165,17 +165,19 @@ def tile_attention_pa_kernel(tc, x, freqs_cis, wq_bytes, wq_scale, wk, wv, out_0
         def shape4(ap):
             return ap.rearrange("p (h j e) -> p h j e", h=NH, e=2)
 
-        def products(c, i):
+        def products(c, i, which):
             u = 4 * c + i // 2
-            if i % 2 == 0:
+            if u not in p1:
                 p1[u] = prod.tile([P, 2, CW], F32, name="p1")
                 p2[u] = prod.tile([P, 2, CW], F32, name="p2")
             full = [P, NH, 64, 2]
             a4 = shape4(acc[c, i])
-            cosb = fc[:, i, :].rearrange("p (j c) -> p j c", c=2)[:, :, 0:1].unsqueeze(1).to_broadcast(full)
-            sinb = s2[:, i, :, :].rearrange("p e j -> p j e").unsqueeze(1).to_broadcast(full)
-            nc.vector.tensor_tensor(out=shape4(p1[u][:, i % 2, :]), in0=cosb, in1=a4, op=MULT)
-            nc.vector.tensor_tensor(out=shape4(p2[u][:, i % 2, :]), in0=sinb, in1=a4[:, :, :, ::-1], op=MULT)
+            if "c" in which:
+                cosb = fc[:, i, :].rearrange("p (j c) -> p j c", c=2)[:, :, 0:1].unsqueeze(1).to_broadcast(full)
+                nc.vector.tensor_tensor(out=shape4(p1[u][:, i % 2, :]), in0=cosb, in1=a4, op=MULT)
+            if "s" in which:
+                sinb = s2[:, i, :, :].rearrange("p e j -> p j e").unsqueeze(1).to_broadcast(full)
+                nc.vector.tensor_tensor(out=shape4(p2[u][:, i % 2, :]), in0=sinb, in1=a4[:, :, :, ::-1], op=MULT)
 
         def add_store(u, eng):
             c, i0 = u // 4, 2 * (u % 4)
@@ -248,9 +250,16 @@ def tile_attention_pa_kernel(tc, x, freqs_cis, wq_bytes, wq_scale, wk, wv, out_0
                 elif op == "M":
                     bank_matmuls(NT * c + int(arg[1:]) if arg[0] == "+" else int(arg))
                 elif op == "K":
-                    products(c, int(arg))
+                    products(c, int(arg), "cs")
+                elif op == "C":
+                    products(c, int(arg), "c")
+                elif op == "D":
+                    products(c - 1 if arg[0] == "-" else c, int(arg[-1]), "s")
                 elif op == "A":
-                    add_store(4 * c + int(arg[0]), arg[2])
+                    if arg[0] == "-":
+                        add_store(4 * (c - 1) + int(arg[1]), arg[3])
+                    else:
+                        add_store(4 * c + int(arg[0]), arg[2])
                 elif op == "B":
                     add_store_bank(c, int(arg[0]), arg[2])
                 elif op == "V":

@@ -25,7 +25,7 @@ FLOPS = 2 * TOKENS * DIM * 3072
 
 LOADS = "k x0 f x1 x2 x3 sc q1 x4 x5 x6 x7 q2 q3 q4 v"
 XGROUPS = ((0, 1), (2, 3), (4, 5, 6, 7))
-HEAD = ("I0.0.S.0.176 I0.0.V.176.512 I0.1.S.0.176 I0.1.V.176.512 T0 E0.S T1 E1.S W0 F T2 E2.S T3 E3.V X0 M0 M1 P P T4 E4.S T5 E5.S K0 X1 M2 M3 T6 P P T7 K1 K2 E6.V E7.V X2 A0.V M4 M5 K3 A1.G M6 M7 P P P P K4 B4.G K5 K6 C7 P* W1 M8 M9 B5.V")
+HEAD = ("Z Z Z Z Z Z Z Z Z I0.0.S.0.176 I0.0.V.176.512 I0.1.S.0.176 I0.1.V.176.512 T0 Z E0.S T1 Z E1.S W0 F T2 E2.S T3 X0 M0 M1 E3.V P P P T4 E4.S T5 E5.S K0 X1 M2 M3 T6 P T7 K1 A0.G K2 E6.V E7.V X2 M4 M5 K3 A1.G M6 M7 P P P P K4 B4.G K5 K6 C7 P* W1 M8 M9 B5.V")
 CHUNK = "D-7 A-3.G P P P M+2 M+3 K0 K1 A0.G P P P M+4 M+5 K2 K3 A1.G P P P M+6 M+7 K4 B4.G K5 P P P K6 C7 P* W+ M+8 M+9 B5.V"
 LAST = "D-7 A-3.G P P M+2 M+3 K0 K1 P* W+ A0.V M+4 M+5 V V K2 V K3 A1.G V M+6 M+7 K4 V V K5 A2.G V V K6 K7 B6.V B7.V"
 BUFS = 4
@@ -80,6 +80,13 @@ def tile_attention_pa_kernel(tc, x, freqs_cis, wq_bytes, wq_scale, wk, wv, out_0
         warm = const.tile([P, 2], F32, name="warm")
         nc.vector.memset(warm[:, 0:1], 0.0)
         nc.scalar.activation(out=warm[:, 1:2], in_=warm[:, 0:1], func=COPY)
+        zeros = const.tile([P, CW], BF16, name="zeros")
+        nc.gpsimd.memset(zeros, 0.0)
+
+        def warm_tensor_engine():
+            scratch = psum_a.tile([P, CW], F32, name="acc")
+            nc.tensor.matmul(out=scratch, lhsT=zeros[:, 0:P], rhs=zeros, start=True, stop=True)
+
         s2 = const.tile([P, NT, 2, 64], BF16, name="s2")
 
         def tables(i0, i1):
@@ -262,6 +269,8 @@ def tile_attention_pa_kernel(tc, x, freqs_cis, wq_bytes, wq_scale, wk, wv, out_0
                         add_store(4 * c + int(arg[0]), arg[2])
                 elif op == "B":
                     add_store_bank(c, int(arg[0]), arg[2])
+                elif op == "Z":
+                    warm_tensor_engine()
                 elif op == "V":
                     value_tile()
                 elif tok == "P":

@@ -24,10 +24,10 @@ NH = 4
 FLOPS = 2 * TOKENS * DIM * 3072
 
 LOADS = "k x0 f x1 x2 x3 sc q1 x4 x5 x6 x7 q2 q3 q4 v"
-XGROUPS = ((0, 1), (2, 3), (4, 5, 6, 7))
-HEAD = ("Z Z Z Z Z Z Z Z Z I0.0.S.0.176 I0.0.V.176.512 I0.1.S.0.176 I0.1.V.176.512 T0 Z E0.S T1 Z E1.S W0 F T2 E2.S T3 X0 M0 M1 E3.V P P P T4 E4.S T5 E5.S K0 X1 M2 M3 T6 P T7 K1 A0.G K2 E6.V E7.V X2 M4 M5 K3 A1.G M6 M7 P P P P K4 B4.G K5 K6 C7 P* W1 M8 M9 B5.V")
-CHUNK = "D-7 A-3.G P P P M+2 M+3 K0 K1 A0.G P P P M+4 M+5 K2 K3 A1.G P P P M+6 M+7 K4 B4.G K5 P P P K6 C7 P* W+ M+8 M+9 B5.V"
-LAST = "D-7 A-3.G P P M+2 M+3 K0 K1 P* W+ A0.V M+4 M+5 V V K2 V K3 A1.G V M+6 M+7 K4 V V K5 A2.G V V K6 K7 B6.V B7.V"
+XGROUPS = ((0, 1), (2, 3), (4, 5), (6, 7))
+HEAD = ("I0.0.S.0.176 I0.0.V.176.512 I0.1.S.0.176 I0.1.V.176.512 T0 E0.S T1 E1.S W0 F T2 E2.S T3 X0 M0 M1 E3.V P P P T4 E4.S T5 E5.S K0 X1 M2 M3 T6 P T7 K1 X2 A0.G M4 M5 K2 E6.V E7.V K3 X3 A1.G M6 M7 P P P P K5 B5.G K4 C7 K6 P* W1 M8 M9 B4.V")
+CHUNK = "D-7 A-3.G P P P M+2 M+3 K0 K1 A0.G P P P M+4 M+5 K3 K2 A1.G P P P M+6 M+7 K5 B5.G K4 P P P C7 K6 P* W+ M+8 M+9 B4.V"
+LAST = "D-7 A-3.G P P M+2 M+3 K0 K1 P* W+ A0.V M+4 M+5 V V K3 V K2 A1.G V M+6 M+7 K5 V V K4 A2.G V V K7 K6 B7.V B6.V"
 BUFS = 4
 
 

@@ -11,24 +11,22 @@ FP8 = mybir.dt.float8_e4m3fn
 FP8X4 = mybir.dt.float8_e4m3fn_x4
 MULT = mybir.AluOpType.mult
 ADD = mybir.AluOpType.add
-SUB = mybir.AluOpType.subtract
 COPY = mybir.ActivationFunctionType.Copy
 
 P = 128
 TOKENS, DIM = 1024, 1024
-NT = TOKENS // P
-NG = DIM // 512
-CW = 512
-HW = CW // 2
-NH = 4
+TILES = TOKENS // P
+PACK = 4
+PASSES = DIM // (P * PACK)
+CHUNK = 512
+HEADS = 4
+HALF = 64
+K_CHUNK = 0
+Q_CHUNKS = (1, 2, 3, 4)
+V_CHUNK = 5
+SCALAR_COLUMNS = 176
+WARM_UP = 9
 FLOPS = 2 * TOKENS * DIM * 3072
-
-LOADS = "k x0 f x1 x2 x3 sc q1 x4 x5 x6 x7 q2 q3 q4 v"
-XGROUPS = ((0, 1), (2, 3), (4, 5), (6, 7))
-HEAD = ("I0.0.S.0.176 I0.0.V.176.512 I0.1.S.0.176 I0.1.V.176.512 T0 E0.S T1 E1.S W0 F T2 E2.S T3 X0 M0 M1 E3.V P P P T4 E4.S T5 E5.S K0 X1 M2 M3 T6 P T7 K1 X2 A0.G M4 M5 K2 E6.V E7.V K3 X3 A1.G M6 M7 P P P P K5 B5.G K4 C7 K6 P* W1 M8 M9 B4.V")
-CHUNK = "D-7 A-3.G P P P M+2 M+3 K0 K1 A0.G P P P M+4 M+5 K3 K2 A1.G P P P M+6 M+7 K5 B5.G K4 P P P C7 K6 P* W+ M+8 M+9 B4.V"
-LAST = "D-7 A-3.G P P M+2 M+3 K0 K1 P* W+ A0.V M+4 M+5 V V K3 V K2 A1.G V M+6 M+7 K5 V V K4 A2.G V V K7 K6 B7.V B6.V"
-BUFS = 4
 
 
 def tile_attention_pa_kernel(tc, x, freqs_cis, wq_bytes, wq_scale, wk, wv, out_0, out_1, out_2):
@@ -36,250 +34,310 @@ def tile_attention_pa_kernel(tc, x, freqs_cis, wq_bytes, wq_scale, wk, wv, out_0
     with ExitStack() as ctx:
         const = ctx.enter_context(tc.tile_pool(name="const", bufs=1))
         raw = ctx.enter_context(tc.tile_pool(name="raw", bufs=1))
-        stage = ctx.enter_context(tc.tile_pool(name="stage", bufs=3))
         codes = ctx.enter_context(tc.tile_pool(name="codes", bufs=1))
-        prod = ctx.enter_context(tc.tile_pool(name="prod", bufs=BUFS))
-        psum_a = ctx.enter_context(tc.psum_pool(name="psum_a", bufs=6))
-        psum_x = ctx.enter_context(tc.psum_pool(name="psum_x", bufs=2))
+        stage = ctx.enter_context(tc.tile_pool(name="stage", bufs=3))
+        prod = ctx.enter_context(tc.tile_pool(name="prod", bufs=4))
+        psum_rope = ctx.enter_context(tc.psum_pool(name="psum_rope", bufs=6))
+        psum_side = ctx.enter_context(tc.psum_pool(name="psum_side", bufs=2))
         ctx.enter_context(tc.manual_schedule())
 
-        wk_v = wk.rearrange("(g p j) n -> g p j n", p=P, j=4)
-        wv_v = wv.rearrange("(g p j) n -> g p j n", p=P, j=4)
-        wq_v = wq_bytes.rearrange("(g p j) n -> g p j n", p=P, j=4)
-        fc_v = freqs_cis.rearrange("(p i) j c -> p i (j c)", i=NT)
-        x_v = x.rearrange("(p i) k -> i p k", i=NT)
-        q_out = out_0.rearrange("(p i) h d -> p i (h d)", i=NT)
-        k_out = out_1.rearrange("(p i) h d -> p i (h d)", i=NT)
-        v_out = out_2.rearrange("(p i) h d -> p i (h d)", i=NT)
+        def k_on_partitions(w):
+            return w.rearrange("(g p t) n -> g p t n", p=P, t=PACK)
 
-        wraw, wqb, x_raw = {}, {}, {}
-        fc = const.tile([P, NT, P], BF16, name="fc")
-        sc = const.tile([P, NG, 4], F32, name="sc")
-        for item in LOADS.split():
-            if item in ("k", "v"):
-                c, view = (0, wk_v) if item == "k" else (5, wv_v)
-                for g in range(NG):
-                    wraw[c, g] = raw.tile([P, 4, CW], BF16, name="wraw%d_%d" % (c, g))
-                    nc.sync.dma_start(out=wraw[c, g], in_=view[g])
-            elif item[0] == "q":
-                c = int(item[1])
-                for g in (range(NG) if len(item) == 2 else (int(item[2]),)):
-                    wqb[c, g] = raw.tile([P, 4, CW], U8, name="wq_bytes%d_%d" % (c, g))
-                    nc.sync.dma_start(out=wqb[c, g], in_=wq_v[g][:, :, (c - 1) * CW:c * CW])
-            elif item[0] == "x":
-                i = int(item[1])
-                x_raw[i] = raw.tile([P, DIM], BF16, name="x_raw%d" % i)
-                nc.sync.dma_start(out=x_raw[i], in_=x_v[i])
-            elif item == "f":
-                nc.sync.dma_start(out=fc, in_=fc_v)
-            else:
-                nc.sync.dma_start(out=sc, in_=wq_scale.rearrange("(g p j) o -> p g (j o)", p=P, j=4))
+        x_tiles = x.rearrange("(p i) k -> i p k", i=TILES)
+        out_of = {K_CHUNK: out_1.rearrange("(p i) h d -> p i (h d)", i=TILES),
+                  V_CHUNK: out_2.rearrange("(p i) h d -> p i (h d)", i=TILES)}
+        for c in Q_CHUNKS:
+            out_of[c] = out_0.rearrange("(p i) h d -> p i (h d)", i=TILES)[:, :, (c - 1) * CHUNK:c * CHUNK]
 
-        ident = const.tile([P, P], F32, name="ident")
-        make_identity(nc, ident[:])
-        warm = const.tile([P, 2], F32, name="warm")
-        nc.vector.memset(warm[:, 0:1], 0.0)
-        nc.scalar.activation(out=warm[:, 1:2], in_=warm[:, 0:1], func=COPY)
-        zeros = const.tile([P, CW], BF16, name="zeros")
+        w_raw, wq_raw, x_raw = {}, {}, {}
+
+        def load_bf16_weights(c, w):
+            for g in range(PASSES):
+                w_raw[c, g] = raw.tile([P, PACK, CHUNK], BF16, name="w_raw%d_%d" % (c, g))
+                nc.sync.dma_start(out=w_raw[c, g], in_=k_on_partitions(w)[g])
+
+        def load_wq_bytes(c):
+            for g in range(PASSES):
+                wq_raw[c, g] = raw.tile([P, PACK, CHUNK], U8, name="wq_bytes%d_%d" % (c, g))
+                nc.sync.dma_start(out=wq_raw[c, g],
+                                  in_=k_on_partitions(wq_bytes)[g][:, :, (c - 1) * CHUNK:c * CHUNK])
+
+        def load_x(i):
+            x_raw[i] = raw.tile([P, DIM], BF16, name="x_raw%d" % i)
+            nc.sync.dma_start(out=x_raw[i], in_=x_tiles[i])
+
+        table = const.tile([P, TILES, 2 * HALF], BF16, name="table")
+        byte_scale = const.tile([P, PASSES, PACK], F32, name="byte_scale")
+        load_bf16_weights(K_CHUNK, wk)
+        load_x(0)
+        nc.sync.dma_start(out=table, in_=freqs_cis.rearrange("(p i) j c -> p i (j c)", i=TILES))
+        for i in (1, 2, 3):
+            load_x(i)
+        nc.sync.dma_start(out=byte_scale, in_=wq_scale.rearrange("(g p t) o -> p g (t o)", p=P, t=PACK))
+        load_wq_bytes(1)
+        for i in (4, 5, 6, 7):
+            load_x(i)
+        for c in (2, 3, 4):
+            load_wq_bytes(c)
+        load_bf16_weights(V_CHUNK, wv)
+
+        identity = const.tile([P, P], F32, name="identity")
+        make_identity(nc, identity[:])
+        first = const.tile([P, 2], F32, name="first")
+        nc.vector.memset(first[:, 0:1], 0.0)
+        nc.scalar.activation(out=first[:, 1:2], in_=first[:, 0:1], func=COPY)
+        signed_sin = const.tile([P, TILES, 2, HALF], BF16, name="signed_sin")
+        zeros = const.tile([P, CHUNK], BF16, name="zeros")
         nc.gpsimd.memset(zeros, 0.0)
 
-        def warm_tensor_engine():
-            scratch = psum_a.tile([P, CW], F32, name="acc")
-            nc.tensor.matmul(out=scratch, lhsT=zeros[:, 0:P], rhs=zeros, start=True, stop=True)
+        def keep_tensor_busy():
+            unread = psum_rope.tile([P, CHUNK], F32, name="bank")
+            nc.tensor.matmul(out=unread, lhsT=zeros[:, 0:P], rhs=zeros, start=True, stop=True)
 
-        s2 = const.tile([P, NT, 2, 64], BF16, name="s2")
+        def make_signed_sin():
+            sin = table.rearrange("p i (j c) -> p i j c", c=2)[:, :, :, 1]
+            nc.vector.tensor_scalar(out=signed_sin[:, :, 0, :], in0=sin, scalar1=-1.0, scalar2=None, op0=MULT)
+            nc.vector.tensor_copy(out=signed_sin[:, :, 1, :], in_=sin)
 
-        def tables(i0, i1):
-            sin = fc[:, i0:i1, :].rearrange("p i (j c) -> p i j c", c=2)[:, :, :, 1]
-            nc.vector.tensor_scalar(out=s2[:, i0:i1, 0, :], in0=sin, scalar1=-1.0, scalar2=None, op0=MULT)
-            nc.vector.tensor_copy(out=s2[:, i0:i1, 1, :], in_=sin)
-
-        xt, xg, xc, xs = {}, {}, {}, {}
+        x_turned, x_grouped, x_codes, x_scales = {}, {}, {}, {}
 
         def x_transpose(i):
-            xt[i] = psum_x.tile([P, NG, 2, P], F32, name="xt")
+            x_turned[i] = psum_side.tile([P, PASSES, 2, P], F32, name="side")
             words = x_raw[i].bitcast(F32)
-            for g in range(NG):
+            for g in range(PASSES):
                 for u in range(2):
-                    nc.tensor.transpose(xt[i][:, g, u, :], words[:, 256 * g + u:256 * (g + 1):2], ident)
+                    nc.tensor.transpose(x_turned[i][:, g, u, :], words[:, 256 * g + u:256 * (g + 1):2], identity)
 
-        where = {}
-        for n, grp in enumerate(XGROUPS):
-            for pos, i in enumerate(grp):
-                where[i] = (n, pos)
+        def x_copy_out(i, engine_copy):
+            if i % 2 == 0:
+                x_grouped[i // 2] = stage.tile([P, 2, PASSES * P * PACK], BF16, name="x_grouped%d" % (i // 2),
+                                               align_bytes=64, bufs=1)
+            words = x_grouped[i // 2][:, i % 2, :].bitcast(F32)
+            engine_copy(out=words.rearrange("p (g r u) -> p g r u", g=PASSES, u=2),
+                        in_=x_turned[i].rearrange("p g u r -> p g r u"))
 
-        def x_evacuate(i, eng):
-            n, pos = where[i]
-            if pos == 0:
-                xg[n] = stage.tile([P, len(XGROUPS[n]), 2 * CW], BF16, name="xg%d" % n, align_bytes=64, bufs=1)
-            dst = xg[n][:, pos, :].bitcast(F32).rearrange("p (g r u) -> p g r u", g=NG, u=2)
-            src = xt[i].rearrange("p g u r -> p g r u")
-            if eng == "V":
-                nc.vector.tensor_copy(out=dst, in_=src)
-            else:
-                nc.scalar.copy(out=dst, in_=src)
+        def x_quantise(d):
+            x_codes[d] = codes.tile([P, 2 * PASSES * P], U32, name="x_codes%d" % d, align_bytes=64)
+            x_scales[d] = codes.tile([P, 2 * PASSES * P], U8, name="x_scales%d" % d, align_bytes=64)
+            nc.vector.quantize_mx(out=x_codes[d].bitcast(FP8X4), scales=x_scales[d],
+                                  in_=x_grouped[d].rearrange("p a k -> p (a k)"))
 
-        def x_quantise(n):
-            width = len(XGROUPS[n]) * NG * P
-            xc[n] = codes.tile([P, width], U32, name="xc%d" % n, align_bytes=64)
-            xs[n] = codes.tile([P, width], U8, name="xs%d" % n, align_bytes=64)
-            nc.vector.quantize_mx(out=xc[n].bitcast(FP8X4), scales=xs[n], in_=xg[n].rearrange("p a k -> p (a k)"))
+        w_wide, w_grouped, w_codes, w_scales = {}, {}, {}, {}
 
-        wg, wc, ws, wide = {}, {}, {}, {}
+        def widen(c, g, t):
+            if t == 0:
+                w_wide[c, g] = stage.tile([P, PACK, CHUNK], BF16, name="w_wide")
+            nc.scalar.activation(out=w_wide[c, g][:, t, :], in_=wq_raw[c, g][:, t, :].bitcast(FP8), func=COPY,
+                                 scale=byte_scale[:, g, t:t + 1])
 
-        def interleave(eng, c, g, n0, n1):
-            if c not in wg:
-                wg[c] = stage.tile([P, NG, CW, 4], BF16, name="wg", align_bytes=64)
-            src = wide[c, g] if (c, g) in wide else wraw[c, g]
-            dst = wg[c][:, g, n0:n1, :]
-            s = src[:, :, n0:n1].rearrange("p t n -> p n t")
-            if eng == "V":
-                nc.vector.tensor_copy(out=dst, in_=s)
-            elif eng == "S":
-                nc.scalar.copy(out=dst, in_=s)
-            else:
-                nc.gpsimd.tensor_scalar(out=dst, in0=s, scalar1=1.0, scalar2=0.0, op0=MULT, op1=ADD)
-
-        def widen(c, g, j):
-            if j == 0:
-                wide[c, g] = stage.tile([P, 4, CW], BF16, name="wide")
-            nc.scalar.activation(out=wide[c, g][:, j, :], in_=wqb[c, g][:, j, :].bitcast(FP8), func=COPY,
-                                 scale=sc[:, g, j:j + 1])
+        def interleave(engine_copy, c, g, n0, n1):
+            if c not in w_grouped:
+                w_grouped[c] = stage.tile([P, PASSES, CHUNK, PACK], BF16, name="w_grouped", align_bytes=64)
+            rows = w_wide[c, g] if c in Q_CHUNKS else w_raw[c, g]
+            engine_copy(out=w_grouped[c][:, g, n0:n1, :], in_=rows[:, :, n0:n1].rearrange("p t n -> p n t"))
 
         def w_quantise(c):
-            wc[c] = codes.tile([P, NG * CW], U32, name="wc%d" % c, align_bytes=64)
-            ws[c] = codes.tile([P, NG * CW], U8, name="ws%d" % c, align_bytes=64)
-            nc.vector.quantize_mx(out=wc[c].bitcast(FP8X4), scales=ws[c],
-                                  in_=wg[c].rearrange("p g n j -> p (g n j)"))
+            w_codes[c] = codes.tile([P, PASSES * CHUNK], U32, name="w_codes%d" % c, align_bytes=64)
+            w_scales[c] = codes.tile([P, PASSES * CHUNK], U8, name="w_scales%d" % c, align_bytes=64)
+            nc.vector.quantize_mx(out=w_codes[c].bitcast(FP8X4), scales=w_scales[c],
+                                  in_=w_grouped[c].rearrange("p g n t -> p (g n t)"))
 
-        def mx(out, c, i, g, n0, n1, start, stop):
-            n, pos = where[i]
-            cols = slice((pos * NG + g) * P, (pos * NG + g + 1) * P)
-            w = slice(g * CW + n0, g * CW + n1)
-            nc.tensor.matmul_mx(out=out, lhsT=xc[n][:, cols].bitcast(FP8X4), lhsT_scale=xs[n][:, cols],
-                                rhs=wc[c][:, w].bitcast(FP8X4), rhs_scale=ws[c][:, w], start=start, stop=stop)
-
-        acc = {}
-
-        def bank_matmuls(b):
-            c, i = b // NT, b % NT
-            acc[c, i] = psum_a.tile([P, CW], F32, name="acc")
-            for g in range(NG):
-                mx(acc[c, i], c, i, g, 0, CW, g == 0, g == NG - 1)
-
-        p1, p2 = {}, {}
-
-        def shape4(ap):
-            return ap.rearrange("p (h j e) -> p h j e", h=NH, e=2)
-
-        def products(c, i, which):
-            u = 4 * c + i // 2
-            if u not in p1:
-                p1[u] = prod.tile([P, 2, CW], F32, name="p1")
-                p2[u] = prod.tile([P, 2, CW], F32, name="p2")
-            full = [P, NH, 64, 2]
-            a4 = shape4(acc[c, i])
-            if "c" in which:
-                cosb = fc[:, i, :].rearrange("p (j c) -> p j c", c=2)[:, :, 0:1].unsqueeze(1).to_broadcast(full)
-                nc.vector.tensor_tensor(out=shape4(p1[u][:, i % 2, :]), in0=cosb, in1=a4, op=MULT)
-            if "s" in which:
-                sinb = s2[:, i, :, :].rearrange("p e j -> p j e").unsqueeze(1).to_broadcast(full)
-                nc.vector.tensor_tensor(out=shape4(p2[u][:, i % 2, :]), in0=sinb, in1=a4[:, :, :, ::-1], op=MULT)
-
-        def add_store(u, eng):
-            c, i0 = u // 4, 2 * (u % 4)
-            o = prod.tile([P, 2, CW], F32, name="o")
-            engine = nc.vector if eng == "V" else nc.gpsimd
-            engine.tensor_tensor(out=o, in0=p1[u], in1=p2[u], op=ADD)
-            dst = k_out[:, i0:i0 + 2, :] if c == 0 else q_out[:, i0:i0 + 2, (c - 1) * CW:c * CW]
-            nc.sync.dma_start(out=dst, in_=o)
-
-        def add_store_bank(c, i, eng):
-            u = 4 * c + i // 2
-            o = prod.tile([P, CW], F32, name="o1")
-            engine = nc.vector if eng == "V" else nc.gpsimd
-            engine.tensor_tensor(out=o, in0=p1[u][:, i % 2, :], in1=p2[u][:, i % 2, :], op=ADD)
-            dst = k_out[:, i, :] if c == 0 else q_out[:, i, (c - 1) * CW:c * CW]
-            nc.sync.dma_start(out=dst, in_=o)
-
-        work = []
-        for c in (1, 2, 3, 4, 5):
-            for g in range(NG):
-                if c < 5:
-                    for j in range(4):
-                        work.append(("widen", c, g, j))
-                for blk in range(2):
-                    work.append(("il", c, g, blk))
+        pieces = []
+        for c in Q_CHUNKS + (V_CHUNK,):
+            for g in range(PASSES):
+                if c in Q_CHUNKS:
+                    for t in range(PACK):
+                        pieces.append(("widen", c, g, t))
+                for half in range(2):
+                    pieces.append(("interleave", c, g, half))
         taken = [0]
 
-        def prep_one():
-            kind, c, g, a = work[taken[0]]
-            taken[0] += 1
-            if kind == "widen":
-                widen(c, g, a)
-            else:
-                interleave("S", c, g, a * HW, (a + 1) * HW)
-
-        def prep_chunk(c):
-            while taken[0] < len(work) and work[taken[0]][1] <= c:
-                prep_one()
-
-        vstate = {"n": 0}
-
-        def value_tile():
-            i = vstate["n"]
-            a = psum_x.tile([P, CW], F32, name="xt")
-            for g in range(NG):
-                mx(a, 5, i, g, 0, CW, g == 0, g == NG - 1)
-            if i % 2 == 0:
-                vstate["o"] = prod.tile([P, 2, CW], F32, name="vo")
-            nc.scalar.copy(out=vstate["o"][:, i % 2, :], in_=a)
-            if i % 2 == 1:
-                nc.scalar.dma_start(out=v_out[:, i - 1:i + 1, :], in_=vstate["o"])
-            vstate["n"] = i + 1
-
-        def run(program, c):
-            for tok in program.split():
-                op, arg = tok[0], tok[1:]
-                if op == "I":
-                    a = arg.split(".")
-                    interleave(a[2], int(a[0]), int(a[1]), int(a[3]), int(a[4]))
-                elif op == "T":
-                    x_transpose(int(arg))
-                elif op == "E":
-                    x_evacuate(int(arg[0]), arg[2])
-                elif op == "X":
-                    x_quantise(int(arg))
-                elif op == "F":
-                    tables(0, NT)
-                elif op == "W":
-                    w_quantise(c + 1 if arg == "+" else int(arg))
-                elif op == "M":
-                    bank_matmuls(NT * c + int(arg[1:]) if arg[0] == "+" else int(arg))
-                elif op == "K":
-                    products(c, int(arg), "cs")
-                elif op == "C":
-                    products(c, int(arg), "c")
-                elif op == "D":
-                    products(c - 1 if arg[0] == "-" else c, int(arg[-1]), "s")
-                elif op == "A":
-                    if arg[0] == "-":
-                        add_store(4 * (c - 1) + int(arg[1]), arg[3])
-                    else:
-                        add_store(4 * c + int(arg[0]), arg[2])
-                elif op == "B":
-                    add_store_bank(c, int(arg[0]), arg[2])
-                elif op == "Z":
-                    warm_tensor_engine()
-                elif op == "V":
-                    value_tile()
-                elif tok == "P":
-                    prep_one()
+        def scalar_prepares(count):
+            for piece in pieces[taken[0]:taken[0] + count]:
+                what, c, g, part = piece
+                if what == "widen":
+                    widen(c, g, part)
                 else:
-                    assert tok == "P*"
-                    prep_chunk(c + 1)
+                    interleave(nc.scalar.copy, c, g, part * CHUNK // 2, (part + 1) * CHUNK // 2)
+            taken[0] += count
 
-        run(HEAD, 0)
+        def project(projection, c, i):
+            for g in range(PASSES):
+                tokens = slice(((i % 2) * PASSES + g) * P, ((i % 2) * PASSES + g + 1) * P)
+                columns = slice(g * CHUNK, (g + 1) * CHUNK)
+                nc.tensor.matmul_mx(out=projection, lhsT=x_codes[i // 2][:, tokens].bitcast(FP8X4),
+                                    lhsT_scale=x_scales[i // 2][:, tokens],
+                                    rhs=w_codes[c][:, columns].bitcast(FP8X4), rhs_scale=w_scales[c][:, columns],
+                                    start=(g == 0), stop=(g == PASSES - 1))
+
+        bank = {}
+
+        def fill_bank(c, i):
+            bank[c, i] = psum_rope.tile([P, CHUNK], F32, name="bank")
+            project(bank[c, i], c, i)
+
+        by_cos, by_sin = {}, {}
+        pair_shape = [P, HEADS, HALF, 2]
+
+        def as_pairs(ap):
+            return ap.rearrange("p (h j e) -> p h j e", h=HEADS, e=2)
+
+        def products_of(c, i):
+            if (c, i // 2) not in by_cos:
+                by_cos[c, i // 2] = prod.tile([P, 2, CHUNK], F32, name="by_cos")
+                by_sin[c, i // 2] = prod.tile([P, 2, CHUNK], F32, name="by_sin")
+            return by_cos[c, i // 2][:, i % 2, :], by_sin[c, i // 2][:, i % 2, :]
+
+        def cos_product(c, i):
+            cos = table[:, i, :].rearrange("p (j c) -> p j c", c=2)[:, :, 0:1]
+            nc.vector.tensor_tensor(out=as_pairs(products_of(c, i)[0]), in0=cos.unsqueeze(1).to_broadcast(pair_shape),
+                                    in1=as_pairs(bank[c, i]), op=MULT)
+
+        def sin_product(c, i):
+            sin = signed_sin[:, i, :, :].rearrange("p e j -> p j e")
+            nc.vector.tensor_tensor(out=as_pairs(products_of(c, i)[1]), in0=sin.unsqueeze(1).to_broadcast(pair_shape),
+                                    in1=as_pairs(bank[c, i])[:, :, :, ::-1], op=MULT)
+
+        def both_products(c, i):
+            cos_product(c, i)
+            sin_product(c, i)
+
+        def sum_duo(engine, c, d):
+            rotated = prod.tile([P, 2, CHUNK], F32, name="rotated_duo")
+            engine.tensor_tensor(out=rotated, in0=by_cos[c, d], in1=by_sin[c, d], op=ADD)
+            nc.sync.dma_start(out=out_of[c][:, 2 * d:2 * d + 2, :], in_=rotated)
+
+        def sum_bank(engine, c, i):
+            rotated = prod.tile([P, CHUNK], F32, name="rotated_bank")
+            engine.tensor_tensor(out=rotated, in0=products_of(c, i)[0], in1=products_of(c, i)[1], op=ADD)
+            nc.sync.dma_start(out=out_of[c][:, i, :], in_=rotated)
+
+        value = {}
+
+        def value_tile(i):
+            projection = psum_side.tile([P, CHUNK], F32, name="side")
+            project(projection, V_CHUNK, i)
+            if i % 2 == 0:
+                value[i // 2] = prod.tile([P, 2, CHUNK], F32, name="value")
+            nc.scalar.copy(out=value[i // 2][:, i % 2, :], in_=projection)
+            if i % 2 == 1:
+                nc.scalar.dma_start(out=out_of[V_CHUNK][:, i - 1:i + 1, :], in_=value[i // 2])
+
+
+        def close_chunk(c):
+            cos_product(c, 7)
+            both_products(c, 6)
+            w_quantise(c + 1)
+            fill_bank(c + 1, 0)
+            fill_bank(c + 1, 1)
+            sum_bank(nc.vector, c, 4)
+
+        def open_chunk(c):
+            sin_product(c - 1, 7)
+            sum_duo(nc.gpsimd, c - 1, 3)
+
+        def third_duo(c):
+            both_products(c, 5)
+            sum_bank(nc.gpsimd, c, 5)
+            both_products(c, 4)
+
+        for n in range(WARM_UP):
+            keep_tensor_busy()
+        for g in range(PASSES):
+            interleave(nc.scalar.copy, K_CHUNK, g, 0, SCALAR_COLUMNS)
+            interleave(nc.vector.tensor_copy, K_CHUNK, g, SCALAR_COLUMNS, CHUNK)
+        for i in (0, 1):
+            x_transpose(i)
+            keep_tensor_busy()
+            x_copy_out(i, nc.scalar.copy)
+        w_quantise(K_CHUNK)
+        make_signed_sin()
+        x_transpose(2)
+        x_copy_out(2, nc.scalar.copy)
+        x_transpose(3)
+        x_quantise(0)
+        fill_bank(K_CHUNK, 0)
+        fill_bank(K_CHUNK, 1)
+        x_copy_out(3, nc.vector.tensor_copy)
+        scalar_prepares(3)
+        for i in (4, 5):
+            x_transpose(i)
+            x_copy_out(i, nc.scalar.copy)
+        both_products(K_CHUNK, 0)
+        x_quantise(1)
+        fill_bank(K_CHUNK, 2)
+        fill_bank(K_CHUNK, 3)
+        x_transpose(6)
+        scalar_prepares(1)
+        x_transpose(7)
+        both_products(K_CHUNK, 1)
+        x_quantise(2)
+        sum_duo(nc.gpsimd, K_CHUNK, 0)
+        fill_bank(K_CHUNK, 4)
+        fill_bank(K_CHUNK, 5)
+        both_products(K_CHUNK, 2)
+        x_copy_out(6, nc.vector.tensor_copy)
+        x_copy_out(7, nc.vector.tensor_copy)
+        both_products(K_CHUNK, 3)
+        x_quantise(3)
+        sum_duo(nc.gpsimd, K_CHUNK, 1)
+        fill_bank(K_CHUNK, 6)
+        fill_bank(K_CHUNK, 7)
+        scalar_prepares(4)
+        third_duo(K_CHUNK)
+        scalar_prepares(4)
+        close_chunk(K_CHUNK)
+
         for c in (1, 2, 3):
-            run(CHUNK, c)
-        run(LAST, 4)
+            open_chunk(c)
+            scalar_prepares(3)
+            fill_bank(c, 2)
+            fill_bank(c, 3)
+            both_products(c, 0)
+            both_products(c, 1)
+            sum_duo(nc.gpsimd, c, 0)
+            scalar_prepares(3)
+            fill_bank(c, 4)
+            fill_bank(c, 5)
+            both_products(c, 3)
+            both_products(c, 2)
+            sum_duo(nc.gpsimd, c, 1)
+            scalar_prepares(3)
+            fill_bank(c, 6)
+            fill_bank(c, 7)
+            third_duo(c)
+            scalar_prepares(3)
+            close_chunk(c)
+
+        open_chunk(4)
+        scalar_prepares(2)
+        fill_bank(4, 2)
+        fill_bank(4, 3)
+        both_products(4, 0)
+        both_products(4, 1)
+        scalar_prepares(2)
+        w_quantise(V_CHUNK)
+        sum_duo(nc.vector, 4, 0)
+        fill_bank(4, 4)
+        fill_bank(4, 5)
+        value_tile(0)
+        value_tile(1)
+        both_products(4, 3)
+        value_tile(2)
+        both_products(4, 2)
+        sum_duo(nc.gpsimd, 4, 1)
+        value_tile(3)
+        fill_bank(4, 6)
+        fill_bank(4, 7)
+        both_products(4, 5)
+        value_tile(4)
+        value_tile(5)
+        both_products(4, 4)
+        sum_duo(nc.gpsimd, 4, 2)
+        value_tile(6)
+        value_tile(7)
+        both_products(4, 7)
+        both_products(4, 6)
+        sum_bank(nc.vector, 4, 7)
+        sum_bank(nc.vector, 4, 6)

@@ -213,6 +213,11 @@ def tile_attention_pa_kernel(tc, x, freqs_cis, wq_bytes, wq_scale, wk, wv, out_0
             engine.tensor_tensor(out=rotated, in0=products_of(c, i)[0], in1=products_of(c, i)[1], op=ADD)
             nc.sync.dma_start(out=out_of[c][:, i, :], in_=rotated)
 
+        unread_word = const.tile([P, 1], U32, name="unread_word")
+
+        def gpsimd_waits_for_codes(fresh):
+            nc.gpsimd.tensor_copy(out=unread_word, in_=fresh[:, 0:1])
+
         value = {}
 
         def value_tile(i):
@@ -307,37 +312,34 @@ def tile_attention_pa_kernel(tc, x, freqs_cis, wq_bytes, wq_scale, wk, wv, out_0
             fill_bank(c, 6)
             fill_bank(c, 7)
             third_duo(c)
-            scalar_prepares(3)
+            scalar_prepares(3 if c < 3 else 7)
             close_chunk(c)
 
+        w_quantise(V_CHUNK)
         open_chunk(4)
-        scalar_prepares(2)
         fill_bank(4, 2)
         fill_bank(4, 3)
-        both_products(4, 0)
-        both_products(4, 1)
-        scalar_prepares(2)
-        w_quantise(V_CHUNK)
-        sum_duo(nc.vector, 4, 0)
-        fill_bank(4, 4)
-        fill_bank(4, 5)
         value_tile(0)
         value_tile(1)
-        both_products(4, 3)
+        both_products(4, 0)
+        both_products(4, 1)
+        sum_duo(nc.gpsimd, 4, 0)
+        fill_bank(4, 4)
+        fill_bank(4, 5)
         value_tile(2)
+        value_tile(3)
+        both_products(4, 3)
         both_products(4, 2)
         sum_duo(nc.gpsimd, 4, 1)
-        value_tile(3)
         fill_bank(4, 6)
         fill_bank(4, 7)
+        for i in (4, 5, 6, 7):
+            value_tile(i)
         both_products(4, 5)
-        value_tile(4)
-        value_tile(5)
         both_products(4, 4)
-        sum_duo(nc.gpsimd, 4, 2)
-        value_tile(6)
-        value_tile(7)
+        sum_bank(nc.gpsimd, 4, 5)
         both_products(4, 7)
         both_products(4, 6)
+        sum_bank(nc.vector, 4, 4)
         sum_bank(nc.vector, 4, 7)
         sum_bank(nc.vector, 4, 6)

@@ -26,6 +26,9 @@ Q_CHUNKS = (1, 2, 3, 4)
 V_CHUNK = 5
 SCALAR_COLUMNS = 176
 WARM_UP = 9
+SUBTRACT = mybir.AluOpType.subtract
+GAUSS_DUO = 3
+LAST_ROTATED = 4
 FLOPS = 2 * TOKENS * DIM * 3072
 
 
@@ -37,7 +40,8 @@ def tile_attention_pa_kernel(tc, x, freqs_cis, wq_bytes, wq_scale, wk, wv, out_0
         codes = ctx.enter_context(tc.tile_pool(name="codes", bufs=1))
         stage = ctx.enter_context(tc.tile_pool(name="stage", bufs=3))
         prod = ctx.enter_context(tc.tile_pool(name="prod", bufs=4))
-        psum_rope = ctx.enter_context(tc.psum_pool(name="psum_rope", bufs=6))
+        psum_rope = ctx.enter_context(tc.psum_pool(name="psum_rope", bufs=5))
+        psum_sum = ctx.enter_context(tc.psum_pool(name="psum_sum", bufs=1))
         psum_side = ctx.enter_context(tc.psum_pool(name="psum_side", bufs=2))
         ctx.enter_context(tc.manual_schedule())
 
@@ -95,6 +99,18 @@ def tile_attention_pa_kernel(tc, x, freqs_cis, wq_bytes, wq_scale, wk, wv, out_0
             unread = psum_rope.tile([P, CHUNK], F32, name="bank")
             nc.tensor.matmul(out=unread, lhsT=zeros[:, 0:P], rhs=zeros, start=True, stop=True)
 
+        mixed = const.tile([P, 2, 2, HALF], F32, name="mixed")
+
+        def three_products(c, d):
+            return d == GAUSS_DUO and c != LAST_ROTATED
+
+        def make_mixed():
+            first = 2 * GAUSS_DUO
+            cos = table.rearrange("p i (j c) -> p i j c", c=2)[:, first:, :, 0]
+            sin = table.rearrange("p i (j c) -> p i j c", c=2)[:, first:, :, 1]
+            nc.vector.scalar_tensor_tensor(out=mixed[:, :, 0, :], in0=cos, scalar=-1.0, in1=sin, op0=MULT, op1=SUBTRACT)
+            nc.vector.tensor_tensor(out=mixed[:, :, 1, :], in0=sin, in1=cos, op=SUBTRACT)
+
         def make_signed_sin():
             sin = table.rearrange("p i (j c) -> p i j c", c=2)[:, :, :, 1]
             nc.vector.tensor_scalar(out=signed_sin[:, :, 0, :], in0=sin, scalar1=-1.0, scalar2=None, op0=MULT)
@@ -135,7 +151,12 @@ def tile_attention_pa_kernel(tc, x, freqs_cis, wq_bytes, wq_scale, wk, wv, out_0
             if c not in w_grouped:
                 w_grouped[c] = stage.tile([P, PASSES, CHUNK, PACK], BF16, name="w_grouped", align_bytes=64)
             rows = w_wide[c, g] if c in Q_CHUNKS else w_raw[c, g]
-            engine_copy(out=w_grouped[c][:, g, n0:n1, :], in_=rows[:, :, n0:n1].rearrange("p t n -> p n t"))
+            if c == V_CHUNK:
+                engine_copy(out=w_grouped[c][:, g, n0:n1, :], in_=rows[:, :, n0:n1].rearrange("p t n -> p n t"))
+            else:
+                e, m0, m1 = n0 // (CHUNK // 2), n0 % (CHUNK // 2), (n1 - 1) % (CHUNK // 2) + 1
+                engine_copy(out=w_grouped[c][:, g, n0:n1, :],
+                            in_=rows.rearrange("p t (m e) -> p e m t", e=2)[:, e, m0:m1, :])
 
         def w_quantise(c):
             w_codes[c] = codes.tile([P, PASSES * CHUNK], U32, name="w_codes%d" % c, align_bytes=64)
@@ -173,9 +194,23 @@ def tile_attention_pa_kernel(tc, x, freqs_cis, wq_bytes, wq_scale, wk, wv, out_0
 
         bank = {}
 
+        both = {}
+
         def fill_bank(c, i):
             bank[c, i] = psum_rope.tile([P, CHUNK], F32, name="bank")
             project(bank[c, i], c, i)
+            if three_products(c, i // 2) and i % 2 == 1:
+                both[c] = psum_sum.tile([P, 2, CHUNK // 2], F32, name="both")
+                for tile in (i - 1, i):
+                    for g in range(PASSES):
+                        tokens = slice(((tile % 2) * PASSES + g) * P, ((tile % 2) * PASSES + g + 1) * P)
+                        for e in range(2):
+                            columns = slice(g * CHUNK + e * CHUNK // 2, g * CHUNK + (e + 1) * CHUNK // 2)
+                            nc.tensor.matmul_mx(out=both[c][:, tile % 2, :],
+                                                lhsT=x_codes[tile // 2][:, tokens].bitcast(FP8X4),
+                                                lhsT_scale=x_scales[tile // 2][:, tokens],
+                                                rhs=w_codes[c][:, columns].bitcast(FP8X4), rhs_scale=w_scales[c][:, columns],
+                                                start=(g == 0 and e == 0), stop=(g == PASSES - 1 and e == 1))
 
         by_cos, by_sin = {}, {}
         pair_shape = [P, HEADS, HALF, 2]
@@ -183,29 +218,50 @@ def tile_attention_pa_kernel(tc, x, freqs_cis, wq_bytes, wq_scale, wk, wv, out_0
         def as_pairs(ap):
             return ap.rearrange("p (h j e) -> p h j e", h=HEADS, e=2)
 
+        def bank_pairs(c, i):
+            return bank[c, i].rearrange("p (e h j) -> p h j e", e=2, h=HEADS)
+
         def products_of(c, i):
-            if (c, i // 2) not in by_cos:
-                by_cos[c, i // 2] = prod.tile([P, 2, CHUNK], F32, name="by_cos")
+            if (c, i // 2) not in by_sin:
+                width = CHUNK // 2 if three_products(c, i // 2) else CHUNK
+                by_cos[c, i // 2] = prod.tile([P, 2, width], F32, name="by_cos")
                 by_sin[c, i // 2] = prod.tile([P, 2, CHUNK], F32, name="by_sin")
             return by_cos[c, i // 2][:, i % 2, :], by_sin[c, i // 2][:, i % 2, :]
 
         def cos_product(c, i):
             cos = table[:, i, :].rearrange("p (j c) -> p j c", c=2)[:, :, 0:1]
             nc.vector.tensor_tensor(out=as_pairs(products_of(c, i)[0]), in0=cos.unsqueeze(1).to_broadcast(pair_shape),
-                                    in1=as_pairs(bank[c, i]), op=MULT)
+                                    in1=bank_pairs(c, i), op=MULT)
 
         def sin_product(c, i):
             sin = signed_sin[:, i, :, :].rearrange("p e j -> p j e")
             nc.vector.tensor_tensor(out=as_pairs(products_of(c, i)[1]), in0=sin.unsqueeze(1).to_broadcast(pair_shape),
-                                    in1=as_pairs(bank[c, i])[:, :, :, ::-1], op=MULT)
+                                    in1=bank_pairs(c, i)[:, :, :, ::-1], op=MULT)
 
         def both_products(c, i):
             cos_product(c, i)
             sin_product(c, i)
 
+        def mixed_product(c, i):
+            factor = mixed[:, i - 2 * GAUSS_DUO, :, :].rearrange("p e j -> p j e")
+            nc.vector.tensor_tensor(out=as_pairs(products_of(c, i)[1]), in0=factor.unsqueeze(1).to_broadcast(pair_shape),
+                                    in1=bank_pairs(c, i)[:, :, :, ::-1], op=MULT)
+
+        def common_product(c):
+            cos = table[:, 2 * GAUSS_DUO:, :].rearrange("p a (j c) -> p a j c", c=2)[:, :, :, 0]
+            shape = [P, 2, HEADS, HALF]
+            nc.vector.tensor_tensor(out=by_cos[c, GAUSS_DUO].rearrange("p a (h j) -> p a h j", h=HEADS),
+                                    in0=cos.unsqueeze(2).to_broadcast(shape),
+                                    in1=both[c].rearrange("p a (h j) -> p a h j", h=HEADS), op=MULT)
+
         def sum_duo(engine, c, d):
             rotated = prod.tile([P, 2, CHUNK], F32, name="rotated_duo")
-            engine.tensor_tensor(out=rotated, in0=by_cos[c, d], in1=by_sin[c, d], op=ADD)
+            if three_products(c, d):
+                engine.tensor_tensor(out=rotated.rearrange("p a (m e) -> p a m e", e=2),
+                                     in0=by_cos[c, d].unsqueeze(3).to_broadcast([P, 2, CHUNK // 2, 2]),
+                                     in1=by_sin[c, d].rearrange("p a (m e) -> p a m e", e=2), op=ADD)
+            else:
+                engine.tensor_tensor(out=rotated, in0=by_cos[c, d], in1=by_sin[c, d], op=ADD)
             nc.sync.dma_start(out=out_of[c][:, 2 * d:2 * d + 2, :], in_=rotated)
 
         def sum_bank(engine, c, i):
@@ -231,15 +287,15 @@ def tile_attention_pa_kernel(tc, x, freqs_cis, wq_bytes, wq_scale, wk, wv, out_0
 
 
         def close_chunk(c):
-            cos_product(c, 7)
-            both_products(c, 6)
+            mixed_product(c, 7)
+            mixed_product(c, 6)
             w_quantise(c + 1)
             fill_bank(c + 1, 0)
             fill_bank(c + 1, 1)
             sum_bank(nc.vector, c, 4)
 
         def open_chunk(c):
-            sin_product(c - 1, 7)
+            common_product(c - 1)
             sum_duo(nc.gpsimd, c - 1, 3)
 
         def third_duo(c):
@@ -251,13 +307,15 @@ def tile_attention_pa_kernel(tc, x, freqs_cis, wq_bytes, wq_scale, wk, wv, out_0
             keep_tensor_busy()
         for g in range(PASSES):
             interleave(nc.scalar.copy, K_CHUNK, g, 0, SCALAR_COLUMNS)
-            interleave(nc.vector.tensor_copy, K_CHUNK, g, SCALAR_COLUMNS, CHUNK)
+            interleave(nc.vector.tensor_copy, K_CHUNK, g, SCALAR_COLUMNS, CHUNK // 2)
+            interleave(nc.vector.tensor_copy, K_CHUNK, g, CHUNK // 2, CHUNK)
         for i in (0, 1):
             x_transpose(i)
             keep_tensor_busy()
             x_copy_out(i, nc.scalar.copy)
         w_quantise(K_CHUNK)
         make_signed_sin()
+        make_mixed()
         x_transpose(2)
         x_copy_out(2, nc.scalar.copy)
         x_transpose(3)

@@ -152,11 +152,12 @@ def tile_attention_pa_kernel(tc, x, freqs_cis, wq_bytes, wq_scale, wk, wv, out_0
                 w_grouped[c] = stage.tile([P, PASSES, CHUNK, PACK], BF16, name="w_grouped", align_bytes=64)
             rows = w_wide[c, g] if c in Q_CHUNKS else w_raw[c, g]
             if c == V_CHUNK:
-                engine_copy(out=w_grouped[c][:, g, n0:n1, :], in_=rows[:, :, n0:n1].rearrange("p t n -> p n t"))
+                engine_copy(out=w_grouped[c][:, g, n0:n1, :].rearrange("p (b i) t -> p b t i", i=4),
+                            in_=rows[:, :, n0:n1].rearrange("p t (b i) -> p b t i", i=4))
             else:
                 e, m0, m1 = n0 // (CHUNK // 2), n0 % (CHUNK // 2), (n1 - 1) % (CHUNK // 2) + 1
-                engine_copy(out=w_grouped[c][:, g, n0:n1, :],
-                            in_=rows.rearrange("p t (m e) -> p e m t", e=2)[:, e, m0:m1, :])
+                engine_copy(out=w_grouped[c][:, g, n0:n1, :].rearrange("p (b i) t -> p b t i", i=4),
+                            in_=rows.rearrange("p t (m e) -> p e t m", e=2)[:, e, :, m0:m1].rearrange("p t (b i) -> p b t i", i=4))
 
         def w_quantise(c):
             w_codes[c] = codes.tile([P, PASSES * CHUNK], U32, name="w_codes%d" % c, align_bytes=64)

@@ -82,9 +82,10 @@ def tile_attention_pa_kernel(tc, x, freqs_cis, wq_bytes, wq_scale, wk, wv, out_0
         load_wq_bytes(1)
         for i in (4, 5, 6, 7):
             load_x(i)
-        for c in (2, 3, 4):
+        for c in (2, 3):
             load_wq_bytes(c)
         load_bf16_weights(V_CHUNK, wv)
+        load_wq_bytes(4)
 
         identity = const.tile([P, P], F32, name="identity")
         make_identity(nc, identity[:])
@@ -166,7 +167,7 @@ def tile_attention_pa_kernel(tc, x, freqs_cis, wq_bytes, wq_scale, wk, wv, out_0
                                   in_=w_grouped[c].rearrange("p g n t -> p (g n t)"))
 
         pieces = []
-        for c in Q_CHUNKS + (V_CHUNK,):
+        for c in (1, 2, 3, V_CHUNK, 4):
             for g in range(PASSES):
                 if c in Q_CHUNKS:
                     for t in range(PACK):
@@ -293,6 +294,8 @@ def tile_attention_pa_kernel(tc, x, freqs_cis, wq_bytes, wq_scale, wk, wv, out_0
             w_quantise(c + 1)
             fill_bank(c + 1, 0)
             fill_bank(c + 1, 1)
+            if c + 1 == 3:
+                w_quantise(V_CHUNK)
             sum_bank(nc.vector, c, 4)
 
         def open_chunk(c):
@@ -353,47 +356,51 @@ def tile_attention_pa_kernel(tc, x, freqs_cis, wq_bytes, wq_scale, wk, wv, out_0
         scalar_prepares(4)
         close_chunk(K_CHUNK)
 
+        pieces_a_duo = {1: (3, 3, 3, 3), 2: (4, 4, 4, 4), 3: (12, 0, 0, 0)}
         for c in (1, 2, 3):
             open_chunk(c)
-            scalar_prepares(3)
+            scalar_prepares(pieces_a_duo[c][0])
             fill_bank(c, 2)
             fill_bank(c, 3)
             both_products(c, 0)
             both_products(c, 1)
             sum_duo(nc.gpsimd, c, 0)
-            scalar_prepares(3)
+            scalar_prepares(pieces_a_duo[c][1])
             fill_bank(c, 4)
             fill_bank(c, 5)
+            if c == 3:
+                value_tile(0)
+                value_tile(1)
             both_products(c, 3)
             both_products(c, 2)
             sum_duo(nc.gpsimd, c, 1)
-            scalar_prepares(3)
+            scalar_prepares(pieces_a_duo[c][2])
             fill_bank(c, 6)
             fill_bank(c, 7)
+            if c == 3:
+                value_tile(2)
+                value_tile(3)
             third_duo(c)
-            scalar_prepares(3 if c < 3 else 7)
+            scalar_prepares(pieces_a_duo[c][3])
             close_chunk(c)
 
-        w_quantise(V_CHUNK)
         open_chunk(4)
         fill_bank(4, 2)
         fill_bank(4, 3)
-        value_tile(0)
-        value_tile(1)
         both_products(4, 0)
         both_products(4, 1)
         sum_duo(nc.gpsimd, 4, 0)
         fill_bank(4, 4)
         fill_bank(4, 5)
-        value_tile(2)
-        value_tile(3)
+        value_tile(4)
+        value_tile(5)
         both_products(4, 3)
         both_products(4, 2)
         sum_duo(nc.gpsimd, 4, 1)
         fill_bank(4, 6)
         fill_bank(4, 7)
-        for i in (4, 5, 6, 7):
-            value_tile(i)
+        value_tile(6)
+        value_tile(7)
         both_products(4, 5)
         both_products(4, 4)
         sum_bank(nc.gpsimd, 4, 5)

@@ -27,7 +27,8 @@ V_CHUNK = 5
 SCALAR_COLUMNS = 176
 WARM_UP = 9
 SUBTRACT = mybir.AluOpType.subtract
-GAUSS_DUO = 3
+GAUSS_DUOS = (2, 3)
+FIRST_GAUSS_TILE = 4
 LAST_ROTATED = 4
 FLOPS = 2 * TOKENS * DIM * 3072
 
@@ -100,13 +101,13 @@ def tile_attention_pa_kernel(tc, x, freqs_cis, wq_bytes, wq_scale, wk, wv, out_0
             unread = psum_rope.tile([P, CHUNK], F32, name="bank")
             nc.tensor.matmul(out=unread, lhsT=zeros[:, 0:P], rhs=zeros, start=True, stop=True)
 
-        mixed = const.tile([P, 2, 2, HALF], F32, name="mixed")
+        mixed = const.tile([P, TILES - FIRST_GAUSS_TILE, 2, HALF], F32, name="mixed")
 
         def three_products(c, d):
-            return d == GAUSS_DUO and c != LAST_ROTATED
+            return d in GAUSS_DUOS and c != LAST_ROTATED
 
         def make_mixed():
-            first = 2 * GAUSS_DUO
+            first = FIRST_GAUSS_TILE
             cos = table.rearrange("p i (j c) -> p i j c", c=2)[:, first:, :, 0]
             sin = table.rearrange("p i (j c) -> p i j c", c=2)[:, first:, :, 1]
             nc.vector.scalar_tensor_tensor(out=mixed[:, :, 0, :], in0=cos, scalar=-1.0, in1=sin, op0=MULT, op1=SUBTRACT)
@@ -202,13 +203,13 @@ def tile_attention_pa_kernel(tc, x, freqs_cis, wq_bytes, wq_scale, wk, wv, out_0
             bank[c, i] = psum_rope.tile([P, CHUNK], F32, name="bank")
             project(bank[c, i], c, i)
             if three_products(c, i // 2) and i % 2 == 1:
-                both[c] = psum_sum.tile([P, 2, CHUNK // 2], F32, name="both")
+                both[c, i // 2] = psum_sum.tile([P, 2, CHUNK // 2], F32, name="both")
                 for tile in (i - 1, i):
                     for g in range(PASSES):
                         tokens = slice(((tile % 2) * PASSES + g) * P, ((tile % 2) * PASSES + g + 1) * P)
                         for e in range(2):
                             columns = slice(g * CHUNK + e * CHUNK // 2, g * CHUNK + (e + 1) * CHUNK // 2)
-                            nc.tensor.matmul_mx(out=both[c][:, tile % 2, :],
+                            nc.tensor.matmul_mx(out=both[c, i // 2][:, tile % 2, :],
                                                 lhsT=x_codes[tile // 2][:, tokens].bitcast(FP8X4),
                                                 lhsT_scale=x_scales[tile // 2][:, tokens],
                                                 rhs=w_codes[c][:, columns].bitcast(FP8X4), rhs_scale=w_scales[c][:, columns],
@@ -245,16 +246,17 @@ def tile_attention_pa_kernel(tc, x, freqs_cis, wq_bytes, wq_scale, wk, wv, out_0
             sin_product(c, i)
 
         def mixed_product(c, i):
-            factor = mixed[:, i - 2 * GAUSS_DUO, :, :].rearrange("p e j -> p j e")
+            factor = mixed[:, i - FIRST_GAUSS_TILE, :, :].rearrange("p e j -> p j e")
             nc.vector.tensor_tensor(out=as_pairs(products_of(c, i)[1]), in0=factor.unsqueeze(1).to_broadcast(pair_shape),
                                     in1=bank_pairs(c, i)[:, :, :, ::-1], op=MULT)
 
-        def common_product(c):
-            cos = table[:, 2 * GAUSS_DUO:, :].rearrange("p a (j c) -> p a j c", c=2)[:, :, :, 0]
+        def common_product(c, d):
+            cos = table[:, 2 * d:2 * d + 2, :].rearrange("p a (j c) -> p a j c", c=2)[:, :, :, 0]
             shape = [P, 2, HEADS, HALF]
-            nc.vector.tensor_tensor(out=by_cos[c, GAUSS_DUO].rearrange("p a (h j) -> p a h j", h=HEADS),
+            products_of(c, 2 * d)
+            nc.vector.tensor_tensor(out=by_cos[c, d].rearrange("p a (h j) -> p a h j", h=HEADS),
                                     in0=cos.unsqueeze(2).to_broadcast(shape),
-                                    in1=both[c].rearrange("p a (h j) -> p a h j", h=HEADS), op=MULT)
+                                    in1=both[c, d].rearrange("p a (h j) -> p a h j", h=HEADS), op=MULT)
 
         def sum_duo(engine, c, d):
             rotated = prod.tile([P, 2, CHUNK], F32, name="rotated_duo")
@@ -296,16 +298,15 @@ def tile_attention_pa_kernel(tc, x, freqs_cis, wq_bytes, wq_scale, wk, wv, out_0
             fill_bank(c + 1, 1)
             if c + 1 == 3:
                 w_quantise(V_CHUNK)
-            sum_bank(nc.vector, c, 4)
+            sum_duo(nc.vector, c, 2)
 
         def open_chunk(c):
-            common_product(c - 1)
+            common_product(c - 1, 3)
             sum_duo(nc.gpsimd, c - 1, 3)
 
         def third_duo(c):
-            both_products(c, 5)
-            sum_bank(nc.gpsimd, c, 5)
-            both_products(c, 4)
+            mixed_product(c, 5)
+            mixed_product(c, 4)
 
         for n in range(WARM_UP):
             keep_tensor_busy()
@@ -350,6 +351,7 @@ def tile_attention_pa_kernel(tc, x, freqs_cis, wq_bytes, wq_scale, wk, wv, out_0
         x_quantise(3)
         sum_duo(nc.gpsimd, K_CHUNK, 1)
         fill_bank(K_CHUNK, 6)
+        common_product(K_CHUNK, 2)
         fill_bank(K_CHUNK, 7)
         scalar_prepares(4)
         third_duo(K_CHUNK)
@@ -376,6 +378,7 @@ def tile_attention_pa_kernel(tc, x, freqs_cis, wq_bytes, wq_scale, wk, wv, out_0
             sum_duo(nc.gpsimd, c, 1)
             scalar_prepares(pieces_a_duo[c][2])
             fill_bank(c, 6)
+            common_product(c, 2)
             fill_bank(c, 7)
             if c == 3:
                 value_tile(2)

@@ -307,6 +307,7 @@ def tile_attention_pa_kernel(tc, x, freqs_cis, wq_bytes, wq_scale, wk, wv, out_0
         def third_duo(c):
             mixed_product(c, 5)
             mixed_product(c, 4)
+            common_product(c, 2)
 
         for n in range(WARM_UP):
             keep_tensor_busy()
@@ -328,7 +329,7 @@ def tile_attention_pa_kernel(tc, x, freqs_cis, wq_bytes, wq_scale, wk, wv, out_0
         fill_bank(K_CHUNK, 0)
         fill_bank(K_CHUNK, 1)
         x_copy_out(3, nc.vector.tensor_copy)
-        scalar_prepares(3)
+        scalar_prepares(4)
         for i in (4, 5):
             x_transpose(i)
             x_copy_out(i, nc.scalar.copy)
@@ -337,10 +338,10 @@ def tile_attention_pa_kernel(tc, x, freqs_cis, wq_bytes, wq_scale, wk, wv, out_0
         fill_bank(K_CHUNK, 2)
         fill_bank(K_CHUNK, 3)
         x_transpose(6)
-        scalar_prepares(1)
         x_transpose(7)
         both_products(K_CHUNK, 1)
         x_quantise(2)
+        gpsimd_waits_for_codes(x_codes[2])
         sum_duo(nc.gpsimd, K_CHUNK, 0)
         fill_bank(K_CHUNK, 4)
         fill_bank(K_CHUNK, 5)
@@ -351,10 +352,9 @@ def tile_attention_pa_kernel(tc, x, freqs_cis, wq_bytes, wq_scale, wk, wv, out_0
         x_quantise(3)
         sum_duo(nc.gpsimd, K_CHUNK, 1)
         fill_bank(K_CHUNK, 6)
-        common_product(K_CHUNK, 2)
-        fill_bank(K_CHUNK, 7)
         scalar_prepares(4)
         third_duo(K_CHUNK)
+        fill_bank(K_CHUNK, 7)
         scalar_prepares(4)
         close_chunk(K_CHUNK)
 
@@ -378,32 +378,31 @@ def tile_attention_pa_kernel(tc, x, freqs_cis, wq_bytes, wq_scale, wk, wv, out_0
             sum_duo(nc.gpsimd, c, 1)
             scalar_prepares(pieces_a_duo[c][2])
             fill_bank(c, 6)
-            common_product(c, 2)
+            third_duo(c)
             fill_bank(c, 7)
             if c == 3:
                 value_tile(2)
                 value_tile(3)
-            third_duo(c)
             scalar_prepares(pieces_a_duo[c][3])
             close_chunk(c)
 
         open_chunk(4)
         fill_bank(4, 2)
         fill_bank(4, 3)
+        value_tile(4)
+        value_tile(5)
         both_products(4, 0)
         both_products(4, 1)
         sum_duo(nc.gpsimd, 4, 0)
         fill_bank(4, 4)
         fill_bank(4, 5)
-        value_tile(4)
-        value_tile(5)
+        value_tile(6)
+        value_tile(7)
         both_products(4, 3)
         both_products(4, 2)
         sum_duo(nc.gpsimd, 4, 1)
         fill_bank(4, 6)
         fill_bank(4, 7)
-        value_tile(6)
-        value_tile(7)
         both_products(4, 5)
         both_products(4, 4)
         sum_bank(nc.gpsimd, 4, 5)

@@ -30,6 +30,7 @@ SUBTRACT = mybir.AluOpType.subtract
 GAUSS_DUOS = (2, 3)
 FIRST_GAUSS_TILE = 4
 LAST_ROTATED = 4
+HELD_BACK = 3
 FLOPS = 2 * TOKENS * DIM * 3072
 
 
@@ -164,8 +165,10 @@ def tile_attention_pa_kernel(tc, x, freqs_cis, wq_bytes, wq_scale, wk, wv, out_0
         def w_quantise(c):
             w_codes[c] = codes.tile([P, PASSES * CHUNK], U32, name="w_codes%d" % c, align_bytes=64)
             w_scales[c] = codes.tile([P, PASSES * CHUNK], U8, name="w_scales%d" % c, align_bytes=64)
-            nc.vector.quantize_mx(out=w_codes[c].bitcast(FP8X4), scales=w_scales[c],
-                                  in_=w_grouped[c].rearrange("p g n t -> p (g n t)"))
+            for g in range(PASSES):
+                columns = slice(g * CHUNK, (g + 1) * CHUNK)
+                nc.vector.quantize_mx(out=w_codes[c][:, columns].bitcast(FP8X4), scales=w_scales[c][:, columns],
+                                      in_=w_grouped[c][:, g, :, :].rearrange("p n t -> p (n t)"))
 
         pieces = []
         for c in (1, 2, 3, V_CHUNK, 4):
@@ -250,13 +253,13 @@ def tile_attention_pa_kernel(tc, x, freqs_cis, wq_bytes, wq_scale, wk, wv, out_0
             nc.vector.tensor_tensor(out=as_pairs(products_of(c, i)[1]), in0=factor.unsqueeze(1).to_broadcast(pair_shape),
                                     in1=bank_pairs(c, i)[:, :, :, ::-1], op=MULT)
 
-        def common_product(c, d):
+        def common_product(c, d, h0=0, h1=HEADS):
             cos = table[:, 2 * d:2 * d + 2, :].rearrange("p a (j c) -> p a j c", c=2)[:, :, :, 0]
-            shape = [P, 2, HEADS, HALF]
+            shape = [P, 2, h1 - h0, HALF]
             products_of(c, 2 * d)
-            nc.vector.tensor_tensor(out=by_cos[c, d].rearrange("p a (h j) -> p a h j", h=HEADS),
+            nc.vector.tensor_tensor(out=by_cos[c, d].rearrange("p a (h j) -> p a h j", h=HEADS)[:, :, h0:h1, :],
                                     in0=cos.unsqueeze(2).to_broadcast(shape),
-                                    in1=both[c, d].rearrange("p a (h j) -> p a h j", h=HEADS), op=MULT)
+                                    in1=both[c, d].rearrange("p a (h j) -> p a h j", h=HEADS)[:, :, h0:h1, :], op=MULT)
 
         def sum_duo(engine, c, d):
             rotated = prod.tile([P, 2, CHUNK], F32, name="rotated_duo")
@@ -293,6 +296,7 @@ def tile_attention_pa_kernel(tc, x, freqs_cis, wq_bytes, wq_scale, wk, wv, out_0
         def close_chunk(c):
             mixed_product(c, 7)
             mixed_product(c, 6)
+            common_product(c, 3, 0, HELD_BACK)
             w_quantise(c + 1)
             fill_bank(c + 1, 0)
             fill_bank(c + 1, 1)
@@ -301,13 +305,13 @@ def tile_attention_pa_kernel(tc, x, freqs_cis, wq_bytes, wq_scale, wk, wv, out_0
             sum_duo(nc.vector, c, 2)
 
         def open_chunk(c):
-            common_product(c - 1, 3)
+            common_product(c - 1, 3, HELD_BACK, HEADS)
             sum_duo(nc.gpsimd, c - 1, 3)
 
         def third_duo(c):
             mixed_product(c, 5)
-            mixed_product(c, 4)
             common_product(c, 2)
+            mixed_product(c, 4)
 
         for n in range(WARM_UP):
             keep_tensor_busy()

@@ -25,7 +25,7 @@ K_CHUNK = 0
 Q_CHUNKS = (1, 2, 3, 4)
 V_CHUNK = 5
 SCALAR_COLUMNS = 176
-WARM_UP = 9
+WARM_UP = 13
 SUBTRACT = mybir.AluOpType.subtract
 GAUSS_DUOS = (2, 3)
 FIRST_GAUSS_TILE = 4

@@ -302,11 +302,10 @@ def tile_attention_pa_kernel(tc, x, freqs_cis, wq_bytes, wq_scale, wk, wv, out_0
             fill_bank(c + 1, 1)
             if c + 1 == 3:
                 w_quantise(V_CHUNK)
+            common_product(c, 3, HELD_BACK, HEADS)
             sum_duo(nc.vector, c, 2)
+            sum_duo(nc.gpsimd, c, 3)
 
-        def open_chunk(c):
-            common_product(c - 1, 3, HELD_BACK, HEADS)
-            sum_duo(nc.gpsimd, c - 1, 3)
 
         def third_duo(c):
             mixed_product(c, 5)
@@ -364,7 +363,6 @@ def tile_attention_pa_kernel(tc, x, freqs_cis, wq_bytes, wq_scale, wk, wv, out_0
 
         pieces_a_duo = {1: (3, 3, 3, 3), 2: (4, 4, 4, 4), 3: (12, 0, 0, 0)}
         for c in (1, 2, 3):
-            open_chunk(c)
             scalar_prepares(pieces_a_duo[c][0])
             fill_bank(c, 2)
             fill_bank(c, 3)
@@ -390,7 +388,6 @@ def tile_attention_pa_kernel(tc, x, freqs_cis, wq_bytes, wq_scale, wk, wv, out_0
             scalar_prepares(pieces_a_duo[c][3])
             close_chunk(c)
 
-        open_chunk(4)
         fill_bank(4, 2)
         fill_bank(4, 3)
         value_tile(4)

from contextlib import ExitStack

import concourse.mybir as mybir
from concourse.masks import make_identity

F32 = mybir.dt.float32
BF16 = mybir.dt.bfloat16
U32 = mybir.dt.uint32
U8 = mybir.dt.uint8
FP8 = mybir.dt.float8_e4m3fn
FP8X4 = mybir.dt.float8_e4m3fn_x4
MULT = mybir.AluOpType.mult
ADD = mybir.AluOpType.add
COPY = mybir.ActivationFunctionType.Copy

P = 128
TOKENS, DIM = 1024, 1024
TILES = TOKENS // P
PACK = 4
PASSES = DIM // (P * PACK)
CHUNK = 512
HEADS = 4
HALF = 64
K_CHUNK = 0
Q_CHUNKS = (1, 2, 3, 4)
V_CHUNK = 5
SCALAR_COLUMNS = 176
WARM_UP = 13
SUBTRACT = mybir.AluOpType.subtract
GAUSS_DUOS = (2, 3)
FIRST_GAUSS_TILE = 4
LAST_ROTATED = 4
HELD_BACK = 3
FLOPS = 2 * TOKENS * DIM * 3072


def tile_attention_pa_kernel(tc, x, freqs_cis, wq_bytes, wq_scale, wk, wv, out_0, out_1, out_2):
    nc = tc.nc
    with ExitStack() as ctx:
        const = ctx.enter_context(tc.tile_pool(name="const", bufs=1))
        raw = ctx.enter_context(tc.tile_pool(name="raw", bufs=1))
        codes = ctx.enter_context(tc.tile_pool(name="codes", bufs=1))
        stage = ctx.enter_context(tc.tile_pool(name="stage", bufs=3))
        prod = ctx.enter_context(tc.tile_pool(name="prod", bufs=4))
        psum_rope = ctx.enter_context(tc.psum_pool(name="psum_rope", bufs=5))
        psum_sum = ctx.enter_context(tc.psum_pool(name="psum_sum", bufs=1))
        psum_side = ctx.enter_context(tc.psum_pool(name="psum_side", bufs=2))
        ctx.enter_context(tc.manual_schedule())

        def k_on_partitions(w):
            return w.rearrange("(g p t) n -> g p t n", p=P, t=PACK)

        x_tiles = x.rearrange("(p i) k -> i p k", i=TILES)
        out_of = {K_CHUNK: out_1.rearrange("(p i) h d -> p i (h d)", i=TILES),
                  V_CHUNK: out_2.rearrange("(p i) h d -> p i (h d)", i=TILES)}
        for c in Q_CHUNKS:
            out_of[c] = out_0.rearrange("(p i) h d -> p i (h d)", i=TILES)[:, :, (c - 1) * CHUNK:c * CHUNK]

        w_raw, wq_raw, x_raw = {}, {}, {}

        def load_bf16_weights(c, w):
            for g in range(PASSES):
                w_raw[c, g] = raw.tile([P, PACK, CHUNK], BF16, name="w_raw%d_%d" % (c, g))
                nc.sync.dma_start(out=w_raw[c, g], in_=k_on_partitions(w)[g])

        def load_wq_bytes(c):
            for g in range(PASSES):
                wq_raw[c, g] = raw.tile([P, PACK, CHUNK], U8, name="wq_bytes%d_%d" % (c, g))
                nc.sync.dma_start(out=wq_raw[c, g],
                                  in_=k_on_partitions(wq_bytes)[g][:, :, (c - 1) * CHUNK:c * CHUNK])

        def load_x(i):
            x_raw[i] = raw.tile([P, DIM], BF16, name="x_raw%d" % i)
            nc.sync.dma_start(out=x_raw[i], in_=x_tiles[i])

        table = const.tile([P, TILES, 2 * HALF], BF16, name="table")
        byte_scale = const.tile([P, PASSES, PACK], F32, name="byte_scale")
        load_bf16_weights(K_CHUNK, wk)
        load_x(0)
        nc.sync.dma_start(out=table, in_=freqs_cis.rearrange("(p i) j c -> p i (j c)", i=TILES))
        for i in (1, 2, 3):
            load_x(i)
        nc.sync.dma_start(out=byte_scale, in_=wq_scale.rearrange("(g p t) o -> p g (t o)", p=P, t=PACK))
        load_wq_bytes(1)
        for i in (4, 5, 6, 7):
            load_x(i)
        for c in (2, 3):
            load_wq_bytes(c)
        load_bf16_weights(V_CHUNK, wv)
        load_wq_bytes(4)

        identity = const.tile([P, P], F32, name="identity")
        make_identity(nc, identity[:])
        first = const.tile([P, 2], F32, name="first")
        nc.vector.memset(first[:, 0:1], 0.0)
        nc.scalar.activation(out=first[:, 1:2], in_=first[:, 0:1], func=COPY)
        signed_sin = const.tile([P, TILES, 2, HALF], BF16, name="signed_sin")
        zeros = const.tile([P, CHUNK], BF16, name="zeros")
        nc.gpsimd.memset(zeros, 0.0)

        def keep_tensor_busy():
            unread = psum_rope.tile([P, CHUNK], F32, name="bank")
            nc.tensor.matmul(out=unread, lhsT=zeros[:, 0:P], rhs=zeros, start=True, stop=True)

        mixed = const.tile([P, TILES - FIRST_GAUSS_TILE, 2, HALF], F32, name="mixed")

        def three_products(c, d):
            return d in GAUSS_DUOS and c != LAST_ROTATED

        def make_mixed():
            first = FIRST_GAUSS_TILE
            cos = table.rearrange("p i (j c) -> p i j c", c=2)[:, first:, :, 0]
            sin = table.rearrange("p i (j c) -> p i j c", c=2)[:, first:, :, 1]
            nc.vector.scalar_tensor_tensor(out=mixed[:, :, 0, :], in0=cos, scalar=-1.0, in1=sin, op0=MULT, op1=SUBTRACT)
            nc.vector.tensor_tensor(out=mixed[:, :, 1, :], in0=sin, in1=cos, op=SUBTRACT)

        def make_signed_sin():
            sin = table.rearrange("p i (j c) -> p i j c", c=2)[:, :, :, 1]
            nc.vector.tensor_scalar(out=signed_sin[:, :, 0, :], in0=sin, scalar1=-1.0, scalar2=None, op0=MULT)
            nc.vector.tensor_copy(out=signed_sin[:, :, 1, :], in_=sin)

        x_turned, x_grouped, x_codes, x_scales = {}, {}, {}, {}

        def x_transpose(i):
            x_turned[i] = psum_side.tile([P, PASSES, 2, P], F32, name="side")
            words = x_raw[i].bitcast(F32)
            for g in range(PASSES):
                for u in range(2):
                    nc.tensor.transpose(x_turned[i][:, g, u, :], words[:, 256 * g + u:256 * (g + 1):2], identity)

        def x_copy_out(i, engine_copy):
            if i % 2 == 0:
                x_grouped[i // 2] = stage.tile([P, 2, PASSES * P * PACK], BF16, name="x_grouped%d" % (i // 2),
                                               align_bytes=64, bufs=1)
            words = x_grouped[i // 2][:, i % 2, :].bitcast(F32)
            engine_copy(out=words.rearrange("p (g r u) -> p g r u", g=PASSES, u=2),
                        in_=x_turned[i].rearrange("p g u r -> p g r u"))

        def x_quantise(d):
            x_codes[d] = codes.tile([P, 2 * PASSES * P], U32, name="x_codes%d" % d, align_bytes=64)
            x_scales[d] = codes.tile([P, 2 * PASSES * P], U8, name="x_scales%d" % d, align_bytes=64)
            nc.vector.quantize_mx(out=x_codes[d].bitcast(FP8X4), scales=x_scales[d],
                                  in_=x_grouped[d].rearrange("p a k -> p (a k)"))

        w_wide, w_grouped, w_codes, w_scales = {}, {}, {}, {}

        def widen(c, g, t):
            if t == 0:
                w_wide[c, g] = stage.tile([P, PACK, CHUNK], BF16, name="w_wide")
            nc.scalar.activation(out=w_wide[c, g][:, t, :], in_=wq_raw[c, g][:, t, :].bitcast(FP8), func=COPY,
                                 scale=byte_scale[:, g, t:t + 1])

        def interleave(engine_copy, c, g, n0, n1):
            if c not in w_grouped:
                w_grouped[c] = stage.tile([P, PASSES, CHUNK, PACK], BF16, name="w_grouped", align_bytes=64)
            rows = w_wide[c, g] if c in Q_CHUNKS else w_raw[c, g]
            if c == V_CHUNK:
                engine_copy(out=w_grouped[c][:, g, n0:n1, :].rearrange("p (b i) t -> p b t i", i=4),
                            in_=rows[:, :, n0:n1].rearrange("p t (b i) -> p b t i", i=4))
            else:
                e, m0, m1 = n0 // (CHUNK // 2), n0 % (CHUNK // 2), (n1 - 1) % (CHUNK // 2) + 1
                engine_copy(out=w_grouped[c][:, g, n0:n1, :].rearrange("p (b i) t -> p b t i", i=4),
                            in_=rows.rearrange("p t (m e) -> p e t m", e=2)[:, e, :, m0:m1].rearrange("p t (b i) -> p b t i", i=4))

        def w_quantise(c):
            w_codes[c] = codes.tile([P, PASSES * CHUNK], U32, name="w_codes%d" % c, align_bytes=64)
            w_scales[c] = codes.tile([P, PASSES * CHUNK], U8, name="w_scales%d" % c, align_bytes=64)
            for g in range(PASSES):
                columns = slice(g * CHUNK, (g + 1) * CHUNK)
                nc.vector.quantize_mx(out=w_codes[c][:, columns].bitcast(FP8X4), scales=w_scales[c][:, columns],
                                      in_=w_grouped[c][:, g, :, :].rearrange("p n t -> p (n t)"))

        pieces = []
        for c in (1, 2, 3, V_CHUNK, 4):
            for g in range(PASSES):
                if c in Q_CHUNKS:
                    for t in range(PACK):
                        pieces.append(("widen", c, g, t))
                for half in range(2):
                    pieces.append(("interleave", c, g, half))
        taken = [0]

        def scalar_prepares(count):
            for piece in pieces[taken[0]:taken[0] + count]:
                what, c, g, part = piece
                if what == "widen":
                    widen(c, g, part)
                else:
                    interleave(nc.scalar.copy, c, g, part * CHUNK // 2, (part + 1) * CHUNK // 2)
            taken[0] += count

        def project(projection, c, i):
            for g in range(PASSES):
                tokens = slice(((i % 2) * PASSES + g) * P, ((i % 2) * PASSES + g + 1) * P)
                columns = slice(g * CHUNK, (g + 1) * CHUNK)
                nc.tensor.matmul_mx(out=projection, lhsT=x_codes[i // 2][:, tokens].bitcast(FP8X4),
                                    lhsT_scale=x_scales[i // 2][:, tokens],
                                    rhs=w_codes[c][:, columns].bitcast(FP8X4), rhs_scale=w_scales[c][:, columns],
                                    start=(g == 0), stop=(g == PASSES - 1))

        bank = {}

        both = {}

        def fill_bank(c, i):
            bank[c, i] = psum_rope.tile([P, CHUNK], F32, name="bank")
            project(bank[c, i], c, i)
            if three_products(c, i // 2) and i % 2 == 1:
                both[c, i // 2] = psum_sum.tile([P, 2, CHUNK // 2], F32, name="both")
                for tile in (i - 1, i):
                    for g in range(PASSES):
                        tokens = slice(((tile % 2) * PASSES + g) * P, ((tile % 2) * PASSES + g + 1) * P)
                        for e in range(2):
                            columns = slice(g * CHUNK + e * CHUNK // 2, g * CHUNK + (e + 1) * CHUNK // 2)
                            nc.tensor.matmul_mx(out=both[c, i // 2][:, tile % 2, :],
                                                lhsT=x_codes[tile // 2][:, tokens].bitcast(FP8X4),
                                                lhsT_scale=x_scales[tile // 2][:, tokens],
                                                rhs=w_codes[c][:, columns].bitcast(FP8X4), rhs_scale=w_scales[c][:, columns],
                                                start=(g == 0 and e == 0), stop=(g == PASSES - 1 and e == 1))

        by_cos, by_sin = {}, {}
        pair_shape = [P, HEADS, HALF, 2]

        def as_pairs(ap):
            return ap.rearrange("p (h j e) -> p h j e", h=HEADS, e=2)

        def bank_pairs(c, i):
            return bank[c, i].rearrange("p (e h j) -> p h j e", e=2, h=HEADS)

        def products_of(c, i):
            if (c, i // 2) not in by_sin:
                width = CHUNK // 2 if three_products(c, i // 2) else CHUNK
                by_cos[c, i // 2] = prod.tile([P, 2, width], F32, name="by_cos")
                by_sin[c, i // 2] = prod.tile([P, 2, CHUNK], F32, name="by_sin")
            return by_cos[c, i // 2][:, i % 2, :], by_sin[c, i // 2][:, i % 2, :]

        def cos_product(c, i):
            cos = table[:, i, :].rearrange("p (j c) -> p j c", c=2)[:, :, 0:1]
            nc.vector.tensor_tensor(out=as_pairs(products_of(c, i)[0]), in0=cos.unsqueeze(1).to_broadcast(pair_shape),
                                    in1=bank_pairs(c, i), op=MULT)

        def sin_product(c, i):
            sin = signed_sin[:, i, :, :].rearrange("p e j -> p j e")
            nc.vector.tensor_tensor(out=as_pairs(products_of(c, i)[1]), in0=sin.unsqueeze(1).to_broadcast(pair_shape),
                                    in1=bank_pairs(c, i)[:, :, :, ::-1], op=MULT)

        def both_products(c, i):
            cos_product(c, i)
            sin_product(c, i)

        def mixed_product(c, i):
            factor = mixed[:, i - FIRST_GAUSS_TILE, :, :].rearrange("p e j -> p j e")
            nc.vector.tensor_tensor(out=as_pairs(products_of(c, i)[1]), in0=factor.unsqueeze(1).to_broadcast(pair_shape),
                                    in1=bank_pairs(c, i)[:, :, :, ::-1], op=MULT)

        def common_product(c, d, h0=0, h1=HEADS):
            cos = table[:, 2 * d:2 * d + 2, :].rearrange("p a (j c) -> p a j c", c=2)[:, :, :, 0]
            shape = [P, 2, h1 - h0, HALF]
            products_of(c, 2 * d)
            nc.vector.tensor_tensor(out=by_cos[c, d].rearrange("p a (h j) -> p a h j", h=HEADS)[:, :, h0:h1, :],
                                    in0=cos.unsqueeze(2).to_broadcast(shape),
                                    in1=both[c, d].rearrange("p a (h j) -> p a h j", h=HEADS)[:, :, h0:h1, :], op=MULT)

        def sum_duo(engine, c, d):
            rotated = prod.tile([P, 2, CHUNK], F32, name="rotated_duo")
            if three_products(c, d):
                engine.tensor_tensor(out=rotated.rearrange("p a (m e) -> p a m e", e=2),
                                     in0=by_cos[c, d].unsqueeze(3).to_broadcast([P, 2, CHUNK // 2, 2]),
                                     in1=by_sin[c, d].rearrange("p a (m e) -> p a m e", e=2), op=ADD)
            else:
                engine.tensor_tensor(out=rotated, in0=by_cos[c, d], in1=by_sin[c, d], op=ADD)
            nc.sync.dma_start(out=out_of[c][:, 2 * d:2 * d + 2, :], in_=rotated)

        def sum_bank(engine, c, i):
            rotated = prod.tile([P, CHUNK], F32, name="rotated_bank")
            engine.tensor_tensor(out=rotated, in0=products_of(c, i)[0], in1=products_of(c, i)[1], op=ADD)
            nc.sync.dma_start(out=out_of[c][:, i, :], in_=rotated)

        unread_word = const.tile([P, 1], U32, name="unread_word")

        def gpsimd_waits_for_codes(fresh):
            nc.gpsimd.tensor_copy(out=unread_word, in_=fresh[:, 0:1])

        value = {}

        def value_tile(i):
            projection = psum_side.tile([P, CHUNK], F32, name="side")
            project(projection, V_CHUNK, i)
            if i % 2 == 0:
                value[i // 2] = prod.tile([P, 2, CHUNK], F32, name="value")
            nc.scalar.copy(out=value[i // 2][:, i % 2, :], in_=projection)
            if i % 2 == 1:
                nc.scalar.dma_start(out=out_of[V_CHUNK][:, i - 1:i + 1, :], in_=value[i // 2])


        def close_chunk(c):
            mixed_product(c, 7)
            mixed_product(c, 6)
            common_product(c, 3, 0, HELD_BACK)
            w_quantise(c + 1)
            fill_bank(c + 1, 0)
            fill_bank(c + 1, 1)
            if c + 1 == 3:
                w_quantise(V_CHUNK)
            common_product(c, 3, HELD_BACK, HEADS)
            sum_duo(nc.vector, c, 2)
            sum_duo(nc.gpsimd, c, 3)


        def third_duo(c):
            mixed_product(c, 5)
            common_product(c, 2)
            mixed_product(c, 4)

        for n in range(WARM_UP):
            keep_tensor_busy()
        for g in range(PASSES):
            interleave(nc.scalar.copy, K_CHUNK, g, 0, SCALAR_COLUMNS)
            interleave(nc.vector.tensor_copy, K_CHUNK, g, SCALAR_COLUMNS, CHUNK // 2)
            interleave(nc.vector.tensor_copy, K_CHUNK, g, CHUNK // 2, CHUNK)
        for i in (0, 1):
            x_transpose(i)
            keep_tensor_busy()
            x_copy_out(i, nc.scalar.copy)
        w_quantise(K_CHUNK)
        make_signed_sin()
        make_mixed()
        x_transpose(2)
        x_copy_out(2, nc.scalar.copy)
        x_transpose(3)
        x_quantise(0)
        fill_bank(K_CHUNK, 0)
        fill_bank(K_CHUNK, 1)
        x_copy_out(3, nc.vector.tensor_copy)
        scalar_prepares(4)
        for i in (4, 5):
            x_transpose(i)
            x_copy_out(i, nc.scalar.copy)
        both_products(K_CHUNK, 0)
        x_quantise(1)
        fill_bank(K_CHUNK, 2)
        fill_bank(K_CHUNK, 3)
        x_transpose(6)
        x_transpose(7)
        both_products(K_CHUNK, 1)
        x_quantise(2)
        gpsimd_waits_for_codes(x_codes[2])
        sum_duo(nc.gpsimd, K_CHUNK, 0)
        fill_bank(K_CHUNK, 4)
        fill_bank(K_CHUNK, 5)
        both_products(K_CHUNK, 2)
        x_copy_out(6, nc.vector.tensor_copy)
        x_copy_out(7, nc.vector.tensor_copy)
        both_products(K_CHUNK, 3)
        x_quantise(3)
        sum_duo(nc.gpsimd, K_CHUNK, 1)
        fill_bank(K_CHUNK, 6)
        scalar_prepares(4)
        third_duo(K_CHUNK)
        fill_bank(K_CHUNK, 7)
        scalar_prepares(4)
        close_chunk(K_CHUNK)

        pieces_a_duo = {1: (3, 3, 3, 3), 2: (4, 4, 4, 4), 3: (12, 0, 0, 0)}
        for c in (1, 2, 3):
            scalar_prepares(pieces_a_duo[c][0])
            fill_bank(c, 2)
            fill_bank(c, 3)
            both_products(c, 0)
            both_products(c, 1)
            sum_duo(nc.gpsimd, c, 0)
            scalar_prepares(pieces_a_duo[c][1])
            fill_bank(c, 4)
            fill_bank(c, 5)
            if c == 3:
                value_tile(0)
                value_tile(1)
            both_products(c, 3)
            both_products(c, 2)
            sum_duo(nc.gpsimd, c, 1)
            scalar_prepares(pieces_a_duo[c][2])
            fill_bank(c, 6)
            third_duo(c)
            fill_bank(c, 7)
            if c == 3:
                value_tile(2)
                value_tile(3)
            scalar_prepares(pieces_a_duo[c][3])
            close_chunk(c)

        fill_bank(4, 2)
        fill_bank(4, 3)
        value_tile(4)
        value_tile(5)
        both_products(4, 0)
        both_products(4, 1)
        sum_duo(nc.gpsimd, 4, 0)
        fill_bank(4, 4)
        fill_bank(4, 5)
        value_tile(6)
        value_tile(7)
        both_products(4, 3)
        both_products(4, 2)
        sum_duo(nc.gpsimd, 4, 1)
        fill_bank(4, 6)
        fill_bank(4, 7)
        both_products(4, 5)
        both_products(4, 4)
        sum_bank(nc.gpsimd, 4, 5)
        both_products(4, 7)
        both_products(4, 6)
        sum_bank(nc.vector, 4, 4)
        sum_bank(nc.vector, 4, 7)
        sum_bank(nc.vector, 4, 6)
